import numpy as np
import ml_dtypes


def mxq(x, axis, fmt="e4m3"):
    dtype, down = {"e4m3": (ml_dtypes.float8_e4m3fn, 7), "e5m2": (ml_dtypes.float8_e5m2, 14)}[fmt]
    v = np.moveaxis(np.asarray(x, np.float32).astype(ml_dtypes.bfloat16).astype(np.float64), axis, -1)
    blocks = v.reshape(v.shape[:-1] + (-1, 32))
    amax = np.abs(blocks).max(-1, keepdims=True)
    byte = np.maximum(np.where(amax > 0, np.frexp(amax)[1] - 1 + 127, 0) - down, 1)
    scale = np.exp2(byte - 127.0)
    codes = (blocks / scale).astype(np.float32).astype(dtype).astype(np.float64)
    return np.moveaxis((codes * scale).reshape(v.shape), -1, axis)


WIDE = False


def mx_kscale(k):
    if not WIDE:
        return np.ones(k)
    levels = np.array([10, -10, 5, -5, 0])
    a = np.random.permutation(np.resize(levels, k // 512 * 4)).reshape(k // 512, 4)
    idx = np.arange(k)
    return np.exp2(a[idx // 512, idx % 128 // 32])


BF16 = ml_dtypes.bfloat16


def bf(x):
    return np.asarray(x, np.float32).astype(BF16)


def f64(x):
    return np.asarray(x).astype(np.float64)


E2M1 = np.array([0.0, 0.5, 1.0, 1.5, 2.0, 3.0, 4.0, 6.0, -0.0, -0.5, -1.0, -1.5, -2.0, -3.0, -4.0, -6.0])


def pack_weight(w, fmt):
    k, n = w.shape
    w = f64(bf(w)).reshape(k // 32, 32, n)
    amax = np.abs(w).max(1)
    if fmt == "e4m3":
        byte = np.frexp(amax)[1] - 1 + 127 - 7
    else:
        mant, ex = np.frexp(amax / 6.0)
        byte = np.where(mant > 0.5, ex, ex - 1) + 127
    byte = np.clip(np.where(amax > 0, byte, 1), 1, 254)
    scaled = (w * np.exp2(127.0 - byte)[:, None, :]).reshape(k, n).astype(np.float32)
    by_word = np.ascontiguousarray(scaled.reshape(k // 512, 128, 4, n).transpose(0, 1, 3, 2))
    if fmt == "e4m3":
        words = by_word.astype(ml_dtypes.float8_e4m3fn).view(np.uint8)
    else:
        c = by_word.astype(ml_dtypes.float4_e2m1fn).view(np.uint8) & 0xF
        words = c[..., 0::2] | (c[..., 1::2] << 4)
    return np.ascontiguousarray(words), np.ascontiguousarray(byte.astype(np.uint8).reshape(k // 512, 16, n))


def unpack_weight(words, scales, fmt):
    g, p, n, _ = words.shape
    if fmt == "e4m3":
        vals = np.ascontiguousarray(words).view(ml_dtypes.float8_e4m3fn).astype(np.float64)
    else:
        nib = np.empty((g, p, n, 4), np.uint8)
        nib[..., 0::2] = words & 0xF
        nib[..., 1::2] = words >> 4
        vals = E2M1[nib]
    vals = vals * np.repeat(np.exp2(scales.astype(np.float64) - 127.0), 8, axis=1)[..., None]
    return vals.transpose(0, 1, 3, 2).reshape(g * 512, n)


B, N, F, U, S = 32, 512, 128, 128, 2
C = S * (F + U)
FMT = "e4m3"


def sigmoid(v):
    return 1.0 / (1.0 + np.exp(-v))


def random_walk():
    a = np.random.uniform(size=(N, N))
    return a / a.sum(axis=1, keepdims=True) * np.sqrt(N)


def setup_inputs():
    s = mx_kscale(N)
    r_prev = bf(sigmoid(np.random.standard_normal((B, U, N))) * np.random.standard_normal((B, U, N)) * s)
    h_diff = bf(np.random.standard_normal((B, N, S * F)))
    u = bf(sigmoid(np.random.standard_normal((B, N, U))))
    state = bf(np.random.standard_normal((B, U * N)))
    s0_words, s0_scales = pack_weight(np.ascontiguousarray((random_walk() / s[None, :]).T), FMT)
    s1_words, s1_scales = pack_weight(np.ascontiguousarray((random_walk() / s[None, :]).T), FMT)
    ck_words, ck_scales = pack_weight(np.random.standard_normal((C, U)) / np.sqrt(C), FMT)
    return {"r_prev": r_prev,
            "h_diff": h_diff,
            "u": u,
            "state": state,
            "support0_words": s0_words,
            "support0_scales": s0_scales,
            "support1_words": s1_words,
            "support1_scales": s1_scales,
            "c_kernel_words": ck_words,
            "c_kernel_scales": ck_scales}


def diffuse(xq, supq):
    return np.concatenate([(xq @ sq.T) for sq in supq], axis=1)


def reference(r_prev, h_diff, u, state, support0_words, support0_scales, support1_words, support1_scales, c_kernel_words, c_kernel_scales):
    supq = (unpack_weight(support0_words, support0_scales, FMT).T, unpack_weight(support1_words, support1_scales, FMT).T)
    c_state = diffuse(mxq(f64(r_prev), 2, "e4m3"), supq).transpose(0, 2, 1)
    hc = np.concatenate([f64(h_diff), c_state], axis=-1)
    c = np.tanh(mxq(hc, 2, "e4m3") @ unpack_weight(c_kernel_words, c_kernel_scales, FMT))
    prev_t = f64(state).reshape(B, U, N).transpose(0, 2, 1)
    ug = f64(u)
    z = ug * prev_t + (1.0 - ug) * c
    return z.reshape(B, U * N)

@@ -1,0 +1,285 @@
+from contextlib import ExitStack
+
+import concourse.mybir as mybir
+from concourse.masks import make_identity
+
+F32 = mybir.dt.float32
+BF16 = mybir.dt.bfloat16
+I32 = mybir.dt.int32
+U32 = mybir.dt.uint32
+U8 = mybir.dt.uint8
+FP8X4 = mybir.dt.float8_e4m3fn_x4
+TANH = mybir.ActivationFunctionType.Tanh
+ALU = mybir.AluOpType
+
+P = 128
+PACK = 4
+BATCH = 32
+NODES = 512
+UNITS = 128
+FEATS = 256
+GROUP = 4
+N_GROUPS = BATCH // GROUP
+QUAD = P // GROUP
+NODE_TILES = NODES // P
+
+FLOPS = 2 * BATCH * UNITS * NODES * NODES * 2 + 2 * BATCH * NODES * (FEATS + 2 * UNITS) * UNITS
+
+
+def tile_gcrnncell_pb_t_kernel(
+    tc,
+    r_prev,
+    h_diff,
+    u,
+    state,
+    support0_words,
+    support0_scales,
+    support1_words,
+    support1_scales,
+    c_kernel_words,
+    c_kernel_scales,
+    out,
+):
+    nc = tc.nc
+    with ExitStack() as stack:
+        const = stack.enter_context(tc.tile_pool(name="const", bufs=1))
+        loads = stack.enter_context(tc.tile_pool(name="loads", bufs=3))
+        work = stack.enter_context(tc.tile_pool(name="work", bufs=2))
+        hpool = stack.enter_context(tc.tile_pool(name="hpool", bufs=8))
+        blend = stack.enter_context(tc.tile_pool(name="blend", bufs=3))
+        psum = stack.enter_context(tc.psum_pool(name="psum", bufs=2))
+
+        ident = const.tile([P, P], F32)
+        make_identity(nc, ident[:])
+
+        w_words = []
+        w_plane = []
+        for i in range(2):
+            words = const.tile([P, NODES * PACK], U8, align_bytes=64, name="w_words%d" % i)
+            plane = const.tile([P, NODES], U8, align_bytes=64, name="w_plane%d" % i)
+            nc.vector.memset(plane[:].bitcast(I32), 0)
+            w_words.append(words)
+            w_plane.append(plane)
+        ckh_words = const.tile([P, 2, UNITS * PACK], U8, align_bytes=64)
+        ckh_plane = const.tile([P, 2, UNITS], U8, align_bytes=64)
+        ckd_words = const.tile([P, 2, GROUP, UNITS * PACK], U8, align_bytes=64)
+        ckd_plane = const.tile([P, 2, GROUP, UNITS], U8, align_bytes=64)
+        nc.vector.memset(ckh_words[:].bitcast(I32), 0)
+        nc.vector.memset(ckh_plane[:].bitcast(I32), 0)
+        nc.vector.memset(ckd_words[:].bitcast(I32), 0)
+        nc.vector.memset(ckd_plane[:].bitcast(I32), 0)
+
+        def load_support(i, words_in, scales_in):
+            nc.sync.dma_start(
+                out=w_words[i][:].bitcast(I32),
+                in_=words_in[0].rearrange("p n t -> p (n t)").bitcast(I32),
+            )
+            rows = scales_in[0].bitcast(I32)
+            for q in range(4):
+                nc.sync.dma_start(
+                    out=w_plane[i][QUAD * q : QUAD * q + 4, :].bitcast(I32),
+                    in_=rows[4 * q : 4 * q + 4, :],
+                )
+
+        def load_c_kernel():
+            words_in = c_kernel_words[0].rearrange("p n t -> p (n t)").bitcast(I32)
+            rows = c_kernel_scales[0].bitcast(I32)
+            for half in range(2):
+                nc.sync.dma_start(
+                    out=ckh_words[64 * half : 64 * half + 64, half, :].bitcast(I32),
+                    in_=words_in[0:64, :],
+                )
+                for q in range(2):
+                    base = 64 * half + QUAD * q
+                    nc.sync.dma_start(
+                        out=ckh_plane[base : base + 4, half, :].bitcast(I32),
+                        in_=rows[4 * q : 4 * q + 4, :],
+                    )
+            for i in range(2):
+                for bq in range(GROUP):
+                    nc.sync.dma_start(
+                        out=ckd_words[QUAD * bq : QUAD * bq + QUAD, i, bq, :].bitcast(I32),
+                        in_=words_in[64 + QUAD * i : 64 + QUAD * i + QUAD, :],
+                    )
+                    nc.sync.dma_start(
+                        out=ckd_plane[QUAD * bq : QUAD * bq + 4, i, bq, :].bitcast(I32),
+                        in_=rows[8 + 4 * i : 12 + 4 * i, :],
+                    )
+
+        r_tiles = {}
+        h_tiles = {}
+        u_tiles = {}
+        st_tiles = {}
+        rq_tiles = {}
+        cq_tiles = {}
+        hq_tiles = {}
+        prev_tiles = {}
+
+        def load_r(g):
+            b0 = GROUP * g
+            r_sb = loads.tile([P, PACK, NODES], BF16)
+            nc.sync.dma_start(
+                out=r_sb[:], in_=r_prev[b0 : b0 + GROUP].rearrange("b (a t) n -> (b a) t n", t=PACK)
+            )
+            r_tiles[g] = r_sb
+
+        def load_rest(g):
+            b0 = GROUP * g
+            h_sb = loads.tile([P, GROUP, NODE_TILES * FEATS], BF16)
+            nc.sync.dma_start(
+                out=h_sb[:], in_=h_diff[b0 : b0 + GROUP].rearrange("b (p x) c -> p b (x c)", x=NODE_TILES)
+            )
+            st_sb = loads.tile([P, GROUP, NODES], BF16)
+            nc.sync.dma_start(
+                out=st_sb[:], in_=state[b0 : b0 + GROUP].rearrange("b (j m) -> j b m", m=NODES)
+            )
+            u_sb = loads.tile([P, GROUP, NODE_TILES * UNITS], BF16)
+            nc.sync.dma_start(
+                out=u_sb[:], in_=u[b0 : b0 + GROUP].rearrange("b (p x) j -> p b (x j)", x=NODE_TILES)
+            )
+            h_tiles[g] = h_sb
+            st_tiles[g] = st_sb
+            u_tiles[g] = u_sb
+
+        def quantise_r(g):
+            r32 = r_tiles[g][:].bitcast(F32)
+            rg = work.tile([P, PACK, P, PACK], BF16, align_bytes=64)
+            rg32 = rg[:].bitcast(F32)
+            for tp in range(2):
+                tps = psum.tile([P, 2, 2, P], F32)
+                for t2 in range(2):
+                    for w in range(2):
+                        nc.tensor.transpose(tps[:, t2, w, :], r32[:, 2 * tp + t2, w : NODES // 2 : 2], ident[:])
+                nc.scalar.copy(out=rg32[:, 2 * tp : 2 * tp + 2, :, :], in_=tps[:].rearrange("p t w c -> p t c w"))
+            rq_words = work.tile([P, PACK * P], U32, align_bytes=64)
+            rq_plane = work.tile([P, PACK * P], U8, align_bytes=64)
+            nc.vector.quantize_mx(
+                out=rq_words[:].bitcast(FP8X4), scales=rq_plane[:], in_=rg[:].rearrange("p t c j -> p (t c j)")
+            )
+            rq_tiles[g] = (rq_words, rq_plane)
+
+        def diffuse(g):
+            rq_words, rq_plane = rq_tiles[g]
+            quantised = []
+            for i in range(2):
+                cg = work.tile([P, NODE_TILES, P, PACK], BF16, align_bytes=64, name="cg%d" % i)
+                for m in range(NODE_TILES):
+                    dps = psum.tile([P, PACK, P], F32)
+                    for t in range(PACK):
+                        nc.tensor.matmul_mx(
+                            out=dps[:, t, :],
+                            lhsT=rq_words[:, P * t : P * t + P].bitcast(FP8X4),
+                            lhsT_scale=rq_plane[:, P * t : P * t + P],
+                            rhs=w_words[i][:, PACK * P * m : PACK * P * (m + 1)].bitcast(FP8X4),
+                            rhs_scale=w_plane[i][:, P * m : P * m + P],
+                            start=True,
+                            stop=True,
+                        )
+                    nc.scalar.copy(
+                        out=cg[:, :, QUAD * m : QUAD * m + QUAD, :],
+                        in_=dps[:].rearrange("p t (c x) -> p x c t", x=NODE_TILES),
+                    )
+                cq_words = work.tile([P, NODES], U32, align_bytes=64, name="cq_words%d" % i)
+                cq_plane = work.tile([P, NODES], U8, align_bytes=64, name="cq_plane%d" % i)
+                nc.vector.quantize_mx(
+                    out=cq_words[:].bitcast(FP8X4), scales=cq_plane[:], in_=cg[:].rearrange("p x c t -> p (x c t)")
+                )
+                quantised.append((cq_words, cq_plane))
+            cq_tiles[g] = quantised
+
+        def quantise_h(g):
+            h32 = h_tiles[g][:].bitcast(F32)
+            for bq in range(GROUP):
+                tps = psum.tile([P, 2, 2, P], F32)
+                for s in range(2):
+                    for w in range(2):
+                        nc.tensor.transpose(
+                            tps[:, s, w, :], h32[:, bq, FEATS * s + w : FEATS * (s + 1) : 2], ident[:]
+                        )
+                hg = work.tile([P, 2, P, PACK], BF16, align_bytes=64)
+                nc.scalar.copy(out=hg[:].bitcast(F32), in_=tps[:].rearrange("p s w c -> p s c w"))
+                hq_words = hpool.tile([P, 2 * P], U32, align_bytes=64)
+                hq_plane = hpool.tile([P, 2 * P], U8, align_bytes=64)
+                nc.vector.quantize_mx(
+                    out=hq_words[:].bitcast(FP8X4), scales=hq_plane[:], in_=hg[:].rearrange("p s c j -> p (s c j)")
+                )
+                hq_tiles[(g, bq)] = (hq_words, hq_plane)
+
+        def transpose_state(g):
+            st32 = st_tiles[g][:].bitcast(F32)
+            for pair in range(GROUP // 2):
+                pps = psum.tile([P, 2, 2, P], F32)
+                for b2 in range(2):
+                    for hh in range(2):
+                        nc.tensor.transpose(pps[:, b2, hh, :], st32[:, 2 * pair + b2, hh : NODES // 2 : 2], ident[:])
+                prev_tiles[(g, pair)] = pps
+
+        def candidate_and_blend(g):
+            for bq in range(GROUP):
+                hq_words, hq_plane = hq_tiles[(g, bq)]
+                cps = psum.tile([P, NODE_TILES, UNITS], F32)
+                for x in range(NODE_TILES):
+                    s, half = divmod(x, 2)
+                    nc.tensor.matmul_mx(
+                        out=cps[:, x, :],
+                        lhsT=hq_words[:, P * s : P * s + P].bitcast(FP8X4),
+                        lhsT_scale=hq_plane[:, P * s : P * s + P],
+                        rhs=ckh_words[:, half, :].bitcast(FP8X4),
+                        rhs_scale=ckh_plane[:, half, :],
+                        start=True,
+                        stop=False,
+                    )
+                    for i in range(2):
+                        cq_words, cq_plane = cq_tiles[g][i]
+                        nc.tensor.matmul_mx(
+                            out=cps[:, x, :],
+                            lhsT=cq_words[:, P * x : P * x + P].bitcast(FP8X4),
+                            lhsT_scale=cq_plane[:, P * x : P * x + P],
+                            rhs=ckd_words[:, i, bq, :].bitcast(FP8X4),
+                            rhs_scale=ckd_plane[:, i, bq, :],
+                            start=False,
+                            stop=(i == 1),
+                        )
+                cand = blend.tile([P, NODE_TILES, UNITS], F32)
+                nc.scalar.activation(out=cand[:], in_=cps[:], func=TANH)
+                pair, b2 = divmod(bq, 2)
+                prev = prev_tiles[(g, pair)][:].bitcast(BF16)[:, b2].rearrange("p h (j e) -> p h e j", e=2)
+                diff = blend.tile([P, NODE_TILES, UNITS], F32)
+                nc.vector.tensor_tensor(
+                    out=diff[:].rearrange("p (h e) j -> p h e j", e=2),
+                    in0=prev,
+                    in1=cand[:].rearrange("p (h e) j -> p h e j", e=2),
+                    op=ALU.subtract,
+                )
+                gated = blend.tile([P, NODE_TILES, UNITS], F32)
+                nc.vector.tensor_tensor(
+                    out=gated[:],
+                    in0=diff[:],
+                    in1=u_tiles[g][:, bq, :].rearrange("p (x j) -> p x j", j=UNITS),
+                    op=ALU.mult,
+                )
+                z = blend.tile([P, NODE_TILES, UNITS], F32)
+                nc.vector.tensor_tensor(out=z[:], in0=gated[:], in1=cand[:], op=ALU.add)
+                nc.sync.dma_start(
+                    out=out[GROUP * g + bq].rearrange("(p f) -> p f", f=NODE_TILES * UNITS),
+                    in_=z[:].rearrange("p x j -> p (x j)"),
+                )
+
+        load_support(0, support0_words, support0_scales)
+        load_r(0)
+        load_support(1, support1_words, support1_scales)
+        load_rest(0)
+        load_c_kernel()
+        load_r(1)
+        load_rest(1)
+        quantise_r(0)
+        for g in range(N_GROUPS):
+            if g + 2 < N_GROUPS:
+                load_r(g + 2)
+                load_rest(g + 2)
+            diffuse(g)
+            if g + 1 < N_GROUPS:
+                quantise_r(g + 1)
+            quantise_h(g)
+            transpose_state(g)
+            candidate_and_blend(g)

@@ -22,6 +22,7 @@ GROUP = 4
 N_GROUPS = BATCH // GROUP
 QUAD = P // GROUP
 NODE_TILES = NODES // P
+R_LEAD = 5
 
 FLOPS = 2 * BATCH * UNITS * NODES * NODES * 2 + 2 * BATCH * NODES * (FEATS + 2 * UNITS) * UNITS
 
@@ -42,12 +43,18 @@ def tile_gcrnncell_pb_t_kernel(
 ):
     nc = tc.nc
     with ExitStack() as stack:
+        stack.enter_context(tc.manual_schedule())
         const = stack.enter_context(tc.tile_pool(name="const", bufs=1))
         loads = stack.enter_context(tc.tile_pool(name="loads", bufs=3))
+        gates = stack.enter_context(tc.tile_pool(name="gates", bufs=4))
         work = stack.enter_context(tc.tile_pool(name="work", bufs=2))
+        cpool = stack.enter_context(tc.tile_pool(name="cpool", bufs=4))
         hpool = stack.enter_context(tc.tile_pool(name="hpool", bufs=8))
-        blend = stack.enter_context(tc.tile_pool(name="blend", bufs=3))
-        psum = stack.enter_context(tc.psum_pool(name="psum", bufs=2))
+        blend = stack.enter_context(tc.tile_pool(name="blend", bufs=5))
+        psum_t = stack.enter_context(tc.psum_pool(name="psum_t", bufs=3))
+        psum_d = stack.enter_context(tc.psum_pool(name="psum_d", bufs=2))
+        psum_c = stack.enter_context(tc.psum_pool(name="psum_c", bufs=2))
+        psum_p = stack.enter_context(tc.psum_pool(name="psum_p", bufs=1))
 
         ident = const.tile([P, P], F32)
         make_identity(nc, ident[:])
@@ -110,176 +117,232 @@ def tile_gcrnncell_pb_t_kernel(
         h_tiles = {}
         u_tiles = {}
         st_tiles = {}
+        rg_tiles = {}
         rq_tiles = {}
+        cg_tiles = {}
         cq_tiles = {}
+        hg_tiles = {}
         hq_tiles = {}
         prev_tiles = {}
+        cps_tiles = {}
+        cand_tiles = {}
+
+        def in_range(g):
+            return 0 <= g < N_GROUPS
 
         def load_r(g):
-            b0 = GROUP * g
             r_sb = loads.tile([P, PACK, NODES], BF16)
             nc.sync.dma_start(
-                out=r_sb[:], in_=r_prev[b0 : b0 + GROUP].rearrange("b (a t) n -> (b a) t n", t=PACK)
+                out=r_sb[:], in_=r_prev[GROUP * g : GROUP * (g + 1)].rearrange("b (a t) n -> (b a) t n", t=PACK)
             )
             r_tiles[g] = r_sb
 
-        def load_rest(g):
-            b0 = GROUP * g
+        def load_h(g):
             h_sb = loads.tile([P, GROUP, NODE_TILES * FEATS], BF16)
             nc.sync.dma_start(
-                out=h_sb[:], in_=h_diff[b0 : b0 + GROUP].rearrange("b (p x) c -> p b (x c)", x=NODE_TILES)
-            )
-            st_sb = loads.tile([P, GROUP, NODES], BF16)
-            nc.sync.dma_start(
-                out=st_sb[:], in_=state[b0 : b0 + GROUP].rearrange("b (j m) -> j b m", m=NODES)
-            )
-            u_sb = loads.tile([P, GROUP, NODE_TILES * UNITS], BF16)
-            nc.sync.dma_start(
-                out=u_sb[:], in_=u[b0 : b0 + GROUP].rearrange("b (p x) j -> p b (x j)", x=NODE_TILES)
+                out=h_sb[:],
+                in_=h_diff[GROUP * g : GROUP * (g + 1)].rearrange("b (p x) c -> p b (x c)", x=NODE_TILES),
             )
             h_tiles[g] = h_sb
+
+        def load_blend_inputs(g):
+            st_sb = gates.tile([P, GROUP, NODES], BF16)
+            nc.sync.dma_start(
+                out=st_sb[:], in_=state[GROUP * g : GROUP * (g + 1)].rearrange("b (j m) -> j b m", m=NODES)
+            )
             st_tiles[g] = st_sb
+            u_sb = gates.tile([P, GROUP, NODE_TILES * UNITS], BF16)
+            nc.sync.dma_start(
+                out=u_sb[:], in_=u[GROUP * g : GROUP * (g + 1)].rearrange("b (p x) j -> p b (x j)", x=NODE_TILES)
+            )
             u_tiles[g] = u_sb
 
-        def quantise_r(g):
+        def transpose_r(g, tp):
+            if tp == 0:
+                rg = work.tile([P, PACK, P, PACK], BF16, align_bytes=64)
+                rg_tiles[g] = rg
             r32 = r_tiles[g][:].bitcast(F32)
-            rg = work.tile([P, PACK, P, PACK], BF16, align_bytes=64)
-            rg32 = rg[:].bitcast(F32)
-            for tp in range(2):
-                tps = psum.tile([P, 2, 2, P], F32)
-                for t2 in range(2):
-                    for w in range(2):
-                        nc.tensor.transpose(tps[:, t2, w, :], r32[:, 2 * tp + t2, w : NODES // 2 : 2], ident[:])
-                nc.scalar.copy(out=rg32[:, 2 * tp : 2 * tp + 2, :, :], in_=tps[:].rearrange("p t w c -> p t c w"))
+            rg32 = rg_tiles[g][:].bitcast(F32)
+            tps = psum_t.tile([P, 2, 2, P], F32)
+            for t2 in range(2):
+                for w in range(2):
+                    nc.tensor.transpose(tps[:, t2, w, :], r32[:, 2 * tp + t2, w : NODES // 2 : 2], ident[:])
+            nc.scalar.copy(out=rg32[:, 2 * tp : 2 * tp + 2, :, :], in_=tps[:].rearrange("p t w c -> p t c w"))
+
+        def quantise_r(g):
             rq_words = work.tile([P, PACK * P], U32, align_bytes=64)
             rq_plane = work.tile([P, PACK * P], U8, align_bytes=64)
             nc.vector.quantize_mx(
-                out=rq_words[:].bitcast(FP8X4), scales=rq_plane[:], in_=rg[:].rearrange("p t c j -> p (t c j)")
+                out=rq_words[:].bitcast(FP8X4),
+                scales=rq_plane[:],
+                in_=rg_tiles[g][:].rearrange("p t c j -> p (t c j)"),
             )
             rq_tiles[g] = (rq_words, rq_plane)
 
-        def diffuse(g):
+        def diffuse_bank(g, i, m):
             rq_words, rq_plane = rq_tiles[g]
-            quantised = []
-            for i in range(2):
-                cg = work.tile([P, NODE_TILES, P, PACK], BF16, align_bytes=64, name="cg%d" % i)
-                for m in range(NODE_TILES):
-                    dps = psum.tile([P, PACK, P], F32)
-                    for t in range(PACK):
-                        nc.tensor.matmul_mx(
-                            out=dps[:, t, :],
-                            lhsT=rq_words[:, P * t : P * t + P].bitcast(FP8X4),
-                            lhsT_scale=rq_plane[:, P * t : P * t + P],
-                            rhs=w_words[i][:, PACK * P * m : PACK * P * (m + 1)].bitcast(FP8X4),
-                            rhs_scale=w_plane[i][:, P * m : P * m + P],
-                            start=True,
-                            stop=True,
-                        )
-                    nc.scalar.copy(
-                        out=cg[:, :, QUAD * m : QUAD * m + QUAD, :],
-                        in_=dps[:].rearrange("p t (c x) -> p x c t", x=NODE_TILES),
-                    )
-                cq_words = work.tile([P, NODES], U32, align_bytes=64, name="cq_words%d" % i)
-                cq_plane = work.tile([P, NODES], U8, align_bytes=64, name="cq_plane%d" % i)
-                nc.vector.quantize_mx(
-                    out=cq_words[:].bitcast(FP8X4), scales=cq_plane[:], in_=cg[:].rearrange("p x c t -> p (x c t)")
+            if m == 0:
+                cg = work.tile([P, NODE_TILES, P, PACK], BF16, align_bytes=64)
+                cg_tiles[(g, i)] = cg
+            dps = psum_d.tile([P, PACK, P], F32)
+            for t in range(PACK):
+                nc.tensor.matmul_mx(
+                    out=dps[:, t, :],
+                    lhsT=rq_words[:, P * t : P * t + P].bitcast(FP8X4),
+                    lhsT_scale=rq_plane[:, P * t : P * t + P],
+                    rhs=w_words[i][:, PACK * P * m : PACK * P * (m + 1)].bitcast(FP8X4),
+                    rhs_scale=w_plane[i][:, P * m : P * m + P],
+                    start=True,
+                    stop=True,
                 )
-                quantised.append((cq_words, cq_plane))
-            cq_tiles[g] = quantised
+            nc.scalar.copy(
+                out=cg_tiles[(g, i)][:, :, QUAD * m : QUAD * m + QUAD, :],
+                in_=dps[:].rearrange("p t (c x) -> p x c t", x=NODE_TILES),
+            )
 
-        def quantise_h(g):
+        def quantise_c(g, i):
+            cq_words = cpool.tile([P, NODES], U32, align_bytes=64)
+            cq_plane = cpool.tile([P, NODES], U8, align_bytes=64)
+            nc.vector.quantize_mx(
+                out=cq_words[:].bitcast(FP8X4),
+                scales=cq_plane[:],
+                in_=cg_tiles[(g, i)][:].rearrange("p x c t -> p (x c t)"),
+            )
+            cq_tiles[(g, i)] = (cq_words, cq_plane)
+
+        def transpose_h(g, bq):
             h32 = h_tiles[g][:].bitcast(F32)
-            for bq in range(GROUP):
-                tps = psum.tile([P, 2, 2, P], F32)
-                for s in range(2):
-                    for w in range(2):
-                        nc.tensor.transpose(
-                            tps[:, s, w, :], h32[:, bq, FEATS * s + w : FEATS * (s + 1) : 2], ident[:]
-                        )
-                hg = work.tile([P, 2, P, PACK], BF16, align_bytes=64)
+            tps = psum_t.tile([P, 2, 2, P], F32)
+            for s in range(2):
+                for w in range(2):
+                    nc.tensor.transpose(tps[:, s, w, :], h32[:, bq, FEATS * s + w : FEATS * (s + 1) : 2], ident[:])
+            hg = work.tile([P, 2, P, PACK], BF16, align_bytes=64, bufs=4)
+            if bq % 2 == 0:
                 nc.scalar.copy(out=hg[:].bitcast(F32), in_=tps[:].rearrange("p s w c -> p s c w"))
-                hq_words = hpool.tile([P, 2 * P], U32, align_bytes=64)
-                hq_plane = hpool.tile([P, 2 * P], U8, align_bytes=64)
-                nc.vector.quantize_mx(
-                    out=hq_words[:].bitcast(FP8X4), scales=hq_plane[:], in_=hg[:].rearrange("p s c j -> p (s c j)")
-                )
-                hq_tiles[(g, bq)] = (hq_words, hq_plane)
+            else:
+                nc.vector.tensor_copy(out=hg[:].bitcast(F32), in_=tps[:].rearrange("p s w c -> p s c w"))
+            hg_tiles[(g, bq)] = hg
 
-        def transpose_state(g):
+        def quantise_h(g, bq):
+            hq_words = hpool.tile([P, 2 * P], U32, align_bytes=64)
+            hq_plane = hpool.tile([P, 2 * P], U8, align_bytes=64)
+            nc.vector.quantize_mx(
+                out=hq_words[:].bitcast(FP8X4),
+                scales=hq_plane[:],
+                in_=hg_tiles[(g, bq)][:].rearrange("p s c j -> p (s c j)"),
+            )
+            hq_tiles[(g, bq)] = (hq_words, hq_plane)
+
+        def transpose_state(g, pair):
             st32 = st_tiles[g][:].bitcast(F32)
-            for pair in range(GROUP // 2):
-                pps = psum.tile([P, 2, 2, P], F32)
-                for b2 in range(2):
-                    for hh in range(2):
-                        nc.tensor.transpose(pps[:, b2, hh, :], st32[:, 2 * pair + b2, hh : NODES // 2 : 2], ident[:])
-                prev_tiles[(g, pair)] = pps
+            pps = psum_p.tile([P, 2, 2, P], F32)
+            for b2 in range(2):
+                for hh in range(2):
+                    nc.tensor.transpose(pps[:, b2, hh, :], st32[:, 2 * pair + b2, hh : NODES // 2 : 2], ident[:])
+            prev_tiles[(g, pair)] = pps
 
-        def candidate_and_blend(g):
-            for bq in range(GROUP):
-                hq_words, hq_plane = hq_tiles[(g, bq)]
-                cps = psum.tile([P, NODE_TILES, UNITS], F32)
-                for x in range(NODE_TILES):
-                    s, half = divmod(x, 2)
+        def candidate_passes(g, bq, s):
+            if s == 0:
+                cps = psum_c.tile([P, NODE_TILES, UNITS], F32)
+                cps_tiles[(g, bq)] = cps
+            cps = cps_tiles[(g, bq)]
+            hq_words, hq_plane = hq_tiles[(g, bq)]
+            for half in range(2):
+                x = 2 * s + half
+                nc.tensor.matmul_mx(
+                    out=cps[:, x, :],
+                    lhsT=hq_words[:, P * s : P * s + P].bitcast(FP8X4),
+                    lhsT_scale=hq_plane[:, P * s : P * s + P],
+                    rhs=ckh_words[:, half, :].bitcast(FP8X4),
+                    rhs_scale=ckh_plane[:, half, :],
+                    start=True,
+                    stop=False,
+                )
+                for i in range(2):
+                    cq_words, cq_plane = cq_tiles[(g, i)]
                     nc.tensor.matmul_mx(
                         out=cps[:, x, :],
-                        lhsT=hq_words[:, P * s : P * s + P].bitcast(FP8X4),
-                        lhsT_scale=hq_plane[:, P * s : P * s + P],
-                        rhs=ckh_words[:, half, :].bitcast(FP8X4),
-                        rhs_scale=ckh_plane[:, half, :],
-                        start=True,
-                        stop=False,
+                        lhsT=cq_words[:, P * x : P * x + P].bitcast(FP8X4),
+                        lhsT_scale=cq_plane[:, P * x : P * x + P],
+                        rhs=ckd_words[:, i, bq, :].bitcast(FP8X4),
+                        rhs_scale=ckd_plane[:, i, bq, :],
+                        start=False,
+                        stop=(i == 1),
                     )
-                    for i in range(2):
-                        cq_words, cq_plane = cq_tiles[g][i]
-                        nc.tensor.matmul_mx(
-                            out=cps[:, x, :],
-                            lhsT=cq_words[:, P * x : P * x + P].bitcast(FP8X4),
-                            lhsT_scale=cq_plane[:, P * x : P * x + P],
-                            rhs=ckd_words[:, i, bq, :].bitcast(FP8X4),
-                            rhs_scale=ckd_plane[:, i, bq, :],
-                            start=False,
-                            stop=(i == 1),
-                        )
-                cand = blend.tile([P, NODE_TILES, UNITS], F32)
-                nc.scalar.activation(out=cand[:], in_=cps[:], func=TANH)
-                pair, b2 = divmod(bq, 2)
-                prev = prev_tiles[(g, pair)][:].bitcast(BF16)[:, b2].rearrange("p h (j e) -> p h e j", e=2)
-                diff = blend.tile([P, NODE_TILES, UNITS], F32)
-                nc.vector.tensor_tensor(
-                    out=diff[:].rearrange("p (h e) j -> p h e j", e=2),
-                    in0=prev,
-                    in1=cand[:].rearrange("p (h e) j -> p h e j", e=2),
-                    op=ALU.subtract,
-                )
-                gated = blend.tile([P, NODE_TILES, UNITS], F32)
-                nc.vector.tensor_tensor(
-                    out=gated[:],
-                    in0=diff[:],
-                    in1=u_tiles[g][:, bq, :].rearrange("p (x j) -> p x j", j=UNITS),
-                    op=ALU.mult,
-                )
-                z = blend.tile([P, NODE_TILES, UNITS], F32)
-                nc.vector.tensor_tensor(out=z[:], in0=gated[:], in1=cand[:], op=ALU.add)
-                nc.sync.dma_start(
-                    out=out[GROUP * g + bq].rearrange("(p f) -> p f", f=NODE_TILES * UNITS),
-                    in_=z[:].rearrange("p x j -> p (x j)"),
-                )
 
-        load_support(0, support0_words, support0_scales)
+        def candidate_tanh(g, bq):
+            cand = blend.tile([P, NODE_TILES, UNITS], F32)
+            nc.scalar.activation(out=cand[:], in_=cps_tiles[(g, bq)][:], func=TANH)
+            cand_tiles[(g, bq)] = cand
+
+        def blend_and_store(g, bq):
+            cand = cand_tiles[(g, bq)]
+            pair, b2 = divmod(bq, 2)
+            prev = prev_tiles[(g, pair)][:].bitcast(BF16)[:, b2].rearrange("p h (j e) -> p h e j", e=2)
+            diff = blend.tile([P, NODE_TILES, UNITS], F32)
+            nc.vector.tensor_tensor(
+                out=diff[:].rearrange("p (h e) j -> p h e j", e=2),
+                in0=prev,
+                in1=cand[:].rearrange("p (h e) j -> p h e j", e=2),
+                op=ALU.subtract,
+            )
+            gated = blend.tile([P, NODE_TILES, UNITS], F32)
+            nc.vector.tensor_tensor(
+                out=gated[:],
+                in0=diff[:],
+                in1=u_tiles[g][:, bq, :].rearrange("p (x j) -> p x j", j=UNITS),
+                op=ALU.mult,
+            )
+            z = blend.tile([P, NODE_TILES, UNITS], F32)
+            nc.gpsimd.tensor_tensor(out=z[:], in0=gated[:], in1=cand[:], op=ALU.add)
+            nc.sync.dma_start(
+                out=out[GROUP * g + bq].rearrange("(p f) -> p f", f=NODE_TILES * UNITS),
+                in_=z[:].rearrange("p x j -> p (x j)"),
+            )
+
         load_r(0)
-        load_support(1, support1_words, support1_scales)
-        load_rest(0)
-        load_c_kernel()
         load_r(1)
-        load_rest(1)
-        quantise_r(0)
-        for g in range(N_GROUPS):
-            if g + 2 < N_GROUPS:
-                load_r(g + 2)
-                load_rest(g + 2)
-            diffuse(g)
-            if g + 1 < N_GROUPS:
-                quantise_r(g + 1)
-            quantise_h(g)
-            transpose_state(g)
-            candidate_and_blend(g)
+        load_support(0, support0_words, support0_scales)
+        load_support(1, support1_words, support1_scales)
+        load_h(0)
+        load_r(2)
+        load_c_kernel()
+        load_blend_inputs(0)
+        load_h(1)
+        for step in range(-R_LEAD, 2 * N_GROUPS):
+            g, i = divmod(step, 2)
+            if i == 0 and g >= -1:
+                if in_range(g + 4):
+                    load_r(g + 4)
+                if in_range(g + 3):
+                    load_h(g + 3)
+                if in_range(g + 2):
+                    load_blend_inputs(g + 2)
+            for bq in (2 * i, 2 * i + 1):
+                for s in range(2):
+                    if in_range(g + 1):
+                        diffuse_bank(g + 1, i, 2 * (bq % 2) + s)
+                    if in_range(g):
+                        candidate_passes(g, bq, s)
+                if in_range(g):
+                    candidate_tanh(g, bq)
+            before_g, before_i = divmod(step - 1, 2)
+            if in_range(before_g):
+                blend_and_store(before_g, 2 * before_i)
+                blend_and_store(before_g, 2 * before_i + 1)
+            if in_range(g + 1):
+                quantise_c(g + 1, i)
+            r_g, r_bank = divmod(step + R_LEAD, 2)
+            if in_range(r_g):
+                transpose_r(r_g, r_bank)
+                if r_bank == 1:
+                    quantise_r(r_g)
+            if in_range(g + 1):
+                transpose_h(g + 1, 2 * i)
+                transpose_h(g + 1, 2 * i + 1)
+                quantise_h(g + 1, 2 * i)
+                quantise_h(g + 1, 2 * i + 1)
+            if in_range(g):
+                transpose_state(g, i)
+        blend_and_store(N_GROUPS - 1, 2)
+        blend_and_store(N_GROUPS - 1, 3)

@@ -76,42 +76,46 @@ def tile_gcrnncell_pb_t_kernel(
         nc.vector.memset(ckd_words[:].bitcast(I32), 0)
         nc.vector.memset(ckd_plane[:].bitcast(I32), 0)
 
-        def load_support(i, words_in, scales_in):
+        def load_support_words(i, words_in):
             nc.sync.dma_start(
                 out=w_words[i][:].bitcast(I32),
                 in_=words_in[0].rearrange("p n t -> p (n t)").bitcast(I32),
             )
-            rows = scales_in[0].bitcast(I32)
-            for q in range(4):
-                nc.sync.dma_start(
-                    out=w_plane[i][QUAD * q : QUAD * q + 4, :].bitcast(I32),
-                    in_=rows[4 * q : 4 * q + 4, :],
-                )
 
-        def load_c_kernel():
+        def load_scale_rows(queue, view, plane_rows, rows):
+            queue.dma_start(out=plane_rows.bitcast(view), in_=rows)
+
+        def load_support_scales(i, scales_in, queue, view):
+            rows = scales_in[0].bitcast(view)
+            for q in range(4):
+                load_scale_rows(queue, view, w_plane[i][QUAD * q : QUAD * q + 4, :], rows[4 * q : 4 * q + 4, :])
+
+        def load_c_kernel_words():
             words_in = c_kernel_words[0].rearrange("p n t -> p (n t)").bitcast(I32)
-            rows = c_kernel_scales[0].bitcast(I32)
             for half in range(2):
                 nc.sync.dma_start(
                     out=ckh_words[64 * half : 64 * half + 64, half, :].bitcast(I32),
                     in_=words_in[0:64, :],
                 )
+            for bq in range(GROUP):
+                nc.sync.dma_start(
+                    out=ckd_words[QUAD * bq : QUAD * bq + QUAD, :, bq, :].bitcast(I32),
+                    in_=words_in[64:P, :].rearrange("(i a) w -> a i w", i=2),
+                )
+
+        def load_c_kernel_scales(queue, view):
+            rows = c_kernel_scales[0].bitcast(view)
+            for half in range(2):
                 for q in range(2):
                     base = 64 * half + QUAD * q
-                    nc.sync.dma_start(
-                        out=ckh_plane[base : base + 4, half, :].bitcast(I32),
-                        in_=rows[4 * q : 4 * q + 4, :],
-                    )
-            for i in range(2):
-                for bq in range(GROUP):
-                    nc.sync.dma_start(
-                        out=ckd_words[QUAD * bq : QUAD * bq + QUAD, i, bq, :].bitcast(I32),
-                        in_=words_in[64 + QUAD * i : 64 + QUAD * i + QUAD, :],
-                    )
-                    nc.sync.dma_start(
-                        out=ckd_plane[QUAD * bq : QUAD * bq + 4, i, bq, :].bitcast(I32),
-                        in_=rows[8 + 4 * i : 12 + 4 * i, :],
-                    )
+                    load_scale_rows(queue, view, ckh_plane[base : base + 4, half, :], rows[4 * q : 4 * q + 4, :])
+            for bq in range(GROUP):
+                load_scale_rows(
+                    queue,
+                    view,
+                    ckd_plane[QUAD * bq : QUAD * bq + 4, :, bq, :],
+                    rows[8:16, :].rearrange("(i r) w -> r i w", i=2),
+                )
 
         r_tiles = {}
         h_tiles = {}
@@ -275,38 +279,47 @@ def tile_gcrnncell_pb_t_kernel(
             nc.scalar.activation(out=cand[:], in_=cps_tiles[(g, bq)][:], func=TANH)
             cand_tiles[(g, bq)] = cand
 
-        def blend_and_store(g, bq):
-            cand = cand_tiles[(g, bq)]
-            pair, b2 = divmod(bq, 2)
-            prev = prev_tiles[(g, pair)][:].bitcast(BF16)[:, b2].rearrange("p h (j e) -> p h e j", e=2)
-            diff = blend.tile([P, NODE_TILES, UNITS], F32)
-            nc.vector.tensor_tensor(
-                out=diff[:].rearrange("p (h e) j -> p h e j", e=2),
-                in0=prev,
-                in1=cand[:].rearrange("p (h e) j -> p h e j", e=2),
-                op=ALU.subtract,
-            )
-            gated = blend.tile([P, NODE_TILES, UNITS], F32)
-            nc.vector.tensor_tensor(
-                out=gated[:],
-                in0=diff[:],
-                in1=u_tiles[g][:, bq, :].rearrange("p (x j) -> p x j", j=UNITS),
-                op=ALU.mult,
-            )
-            z = blend.tile([P, NODE_TILES, UNITS], F32)
-            nc.gpsimd.tensor_tensor(out=z[:], in0=gated[:], in1=cand[:], op=ALU.add)
-            nc.sync.dma_start(
-                out=out[GROUP * g + bq].rearrange("(p f) -> p f", f=NODE_TILES * UNITS),
-                in_=z[:].rearrange("p x j -> p (x j)"),
-            )
+        def blend_and_store(g, pair):
+            batches = (2 * pair, 2 * pair + 1)
+            prev_words = prev_tiles[(g, pair)][:].bitcast(BF16)
+            diffs = {}
+            for bq in batches:
+                diff = blend.tile([P, NODE_TILES, UNITS], F32)
+                nc.vector.tensor_tensor(
+                    out=diff[:].rearrange("p (h e) j -> p h e j", e=2),
+                    in0=prev_words[:, bq % 2].rearrange("p h (j e) -> p h e j", e=2),
+                    in1=cand_tiles[(g, bq)][:].rearrange("p (h e) j -> p h e j", e=2),
+                    op=ALU.subtract,
+                )
+                diffs[bq] = diff
+            gateds = {}
+            for bq in batches:
+                gated = blend.tile([P, NODE_TILES, UNITS], F32)
+                nc.vector.tensor_tensor(
+                    out=gated[:],
+                    in0=diffs[bq][:],
+                    in1=u_tiles[g][:, bq, :].rearrange("p (x j) -> p x j", j=UNITS),
+                    op=ALU.mult,
+                )
+                gateds[bq] = gated
+            for bq in batches:
+                z = blend.tile([P, NODE_TILES, UNITS], F32)
+                nc.gpsimd.tensor_tensor(out=z[:], in0=gateds[bq][:], in1=cand_tiles[(g, bq)][:], op=ALU.add)
+                nc.sync.dma_start(
+                    out=out[GROUP * g + bq].rearrange("(p f) -> p f", f=NODE_TILES * UNITS),
+                    in_=z[:].rearrange("p x j -> p (x j)"),
+                )
 
         load_r(0)
+        load_support_words(0, support0_words)
+        load_support_scales(0, support0_scales, nc.sync, I32)
         load_r(1)
-        load_support(0, support0_words, support0_scales)
-        load_support(1, support1_words, support1_scales)
         load_h(0)
+        load_support_words(1, support1_words)
+        load_support_scales(1, support1_scales, nc.gpsimd, F32)
+        load_c_kernel_scales(nc.gpsimd, F32)
         load_r(2)
-        load_c_kernel()
+        load_c_kernel_words()
         load_blend_inputs(0)
         load_h(1)
         for step in range(-R_LEAD, 2 * N_GROUPS):
@@ -328,8 +341,7 @@ def tile_gcrnncell_pb_t_kernel(
                     candidate_tanh(g, bq)
             before_g, before_i = divmod(step - 1, 2)
             if in_range(before_g):
-                blend_and_store(before_g, 2 * before_i)
-                blend_and_store(before_g, 2 * before_i + 1)
+                blend_and_store(before_g, before_i)
             if in_range(g + 1):
                 quantise_c(g + 1, i)
             r_g, r_bank = divmod(step + R_LEAD, 2)
@@ -344,5 +356,4 @@ def tile_gcrnncell_pb_t_kernel(
                 quantise_h(g + 1, 2 * i + 1)
             if in_range(g):
                 transpose_state(g, i)
-        blend_and_store(N_GROUPS - 1, 2)
-        blend_and_store(N_GROUPS - 1, 3)
+        blend_and_store(N_GROUPS - 1, 1)

@@ -23,6 +23,7 @@ N_GROUPS = BATCH // GROUP
 QUAD = P // GROUP
 NODE_TILES = NODES // P
 R_LEAD = 5
+LOAD_AHEAD = 4
 
 FLOPS = 2 * BATCH * UNITS * NODES * NODES * 2 + 2 * BATCH * NODES * (FEATS + 2 * UNITS) * UNITS
 
@@ -45,8 +46,7 @@ def tile_gcrnncell_pb_t_kernel(
     with ExitStack() as stack:
         stack.enter_context(tc.manual_schedule())
         const = stack.enter_context(tc.tile_pool(name="const", bufs=1))
-        loads = stack.enter_context(tc.tile_pool(name="loads", bufs=3))
-        gates = stack.enter_context(tc.tile_pool(name="gates", bufs=4))
+        loads = stack.enter_context(tc.tile_pool(name="loads", bufs=LOAD_AHEAD + 3))
         work = stack.enter_context(tc.tile_pool(name="work", bufs=2))
         cpool = stack.enter_context(tc.tile_pool(name="cpool", bufs=4))
         hpool = stack.enter_context(tc.tile_pool(name="hpool", bufs=8))
@@ -134,43 +134,46 @@ def tile_gcrnncell_pb_t_kernel(
         def in_range(g):
             return 0 <= g < N_GROUPS
 
-        def load_r(g):
-            r_sb = loads.tile([P, PACK, NODES], BF16)
-            nc.sync.dma_start(
-                out=r_sb[:], in_=r_prev[GROUP * g : GROUP * (g + 1)].rearrange("b (a t) n -> (b a) t n", t=PACK)
-            )
-            r_tiles[g] = r_sb
-
-        def load_h(g):
-            h_sb = loads.tile([P, GROUP, NODE_TILES * FEATS], BF16)
-            nc.sync.dma_start(
-                out=h_sb[:],
-                in_=h_diff[GROUP * g : GROUP * (g + 1)].rearrange("b (p x) c -> p b (x c)", x=NODE_TILES),
-            )
-            h_tiles[g] = h_sb
-
-        def load_blend_inputs(g):
-            st_sb = gates.tile([P, GROUP, NODES], BF16)
-            nc.sync.dma_start(
-                out=st_sb[:], in_=state[GROUP * g : GROUP * (g + 1)].rearrange("b (j m) -> j b m", m=NODES)
-            )
-            st_tiles[g] = st_sb
-            u_sb = gates.tile([P, GROUP, NODE_TILES * UNITS], BF16)
-            nc.sync.dma_start(
-                out=u_sb[:], in_=u[GROUP * g : GROUP * (g + 1)].rearrange("b (p x) j -> p b (x j)", x=NODE_TILES)
-            )
-            u_tiles[g] = u_sb
+        def load_for_step(step):
+            g, tp = divmod(step + R_LEAD, 2)
+            if in_range(g):
+                r_sb = loads.tile([P, 2, NODES], BF16)
+                rows = r_prev[GROUP * g : GROUP * (g + 1)].rearrange("b (a t) n -> (b a) t n", t=PACK)
+                nc.sync.dma_start(out=r_sb[:], in_=rows[:, 2 * tp : 2 * tp + 2, :])
+                r_tiles[(g, tp)] = r_sb
+            g, pair = divmod(step + 2, 2)
+            if in_range(g):
+                b0 = GROUP * g + 2 * pair
+                h_sb = loads.tile([P, 2, NODE_TILES * FEATS], BF16)
+                nc.sync.dma_start(
+                    out=h_sb[:], in_=h_diff[b0 : b0 + 2].rearrange("b (p x) c -> p b (x c)", x=NODE_TILES)
+                )
+                h_tiles[(g, pair)] = h_sb
+            g, pair = divmod(step, 2)
+            if in_range(g):
+                b0 = GROUP * g + 2 * pair
+                st_sb = loads.tile([P, 2, NODES], BF16)
+                nc.sync.dma_start(out=st_sb[:], in_=state[b0 : b0 + 2].rearrange("b (j m) -> j b m", m=NODES))
+                st_tiles[(g, pair)] = st_sb
+            g, pair = divmod(step - 1, 2)
+            if in_range(g):
+                b0 = GROUP * g + 2 * pair
+                u_sb = loads.tile([P, 2, NODE_TILES * UNITS], BF16)
+                nc.sync.dma_start(
+                    out=u_sb[:], in_=u[b0 : b0 + 2].rearrange("b (p x) j -> p b (x j)", x=NODE_TILES)
+                )
+                u_tiles[(g, pair)] = u_sb
 
         def transpose_r(g, tp):
             if tp == 0:
                 rg = work.tile([P, PACK, P, PACK], BF16, align_bytes=64)
                 rg_tiles[g] = rg
-            r32 = r_tiles[g][:].bitcast(F32)
+            r32 = r_tiles[(g, tp)][:].bitcast(F32)
             rg32 = rg_tiles[g][:].bitcast(F32)
             tps = psum_t.tile([P, 2, 2, P], F32)
             for t2 in range(2):
                 for w in range(2):
-                    nc.tensor.transpose(tps[:, t2, w, :], r32[:, 2 * tp + t2, w : NODES // 2 : 2], ident[:])
+                    nc.tensor.transpose(tps[:, t2, w, :], r32[:, t2, w : NODES // 2 : 2], ident[:])
             nc.scalar.copy(out=rg32[:, 2 * tp : 2 * tp + 2, :, :], in_=tps[:].rearrange("p t w c -> p t c w"))
 
         def quantise_r(g):
@@ -215,11 +218,11 @@ def tile_gcrnncell_pb_t_kernel(
             cq_tiles[(g, i)] = (cq_words, cq_plane)
 
         def transpose_h(g, bq):
-            h32 = h_tiles[g][:].bitcast(F32)
+            h32 = h_tiles[(g, bq // 2)][:].bitcast(F32)
             tps = psum_t.tile([P, 2, 2, P], F32)
             for s in range(2):
                 for w in range(2):
-                    nc.tensor.transpose(tps[:, s, w, :], h32[:, bq, FEATS * s + w : FEATS * (s + 1) : 2], ident[:])
+                    nc.tensor.transpose(tps[:, s, w, :], h32[:, bq % 2, FEATS * s + w : FEATS * (s + 1) : 2], ident[:])
             hg = work.tile([P, 2, P, PACK], BF16, align_bytes=64, bufs=4)
             if bq % 2 == 0:
                 nc.scalar.copy(out=hg[:].bitcast(F32), in_=tps[:].rearrange("p s w c -> p s c w"))
@@ -238,11 +241,11 @@ def tile_gcrnncell_pb_t_kernel(
             hq_tiles[(g, bq)] = (hq_words, hq_plane)
 
         def transpose_state(g, pair):
-            st32 = st_tiles[g][:].bitcast(F32)
+            st32 = st_tiles[(g, pair)][:].bitcast(F32)
             pps = psum_p.tile([P, 2, 2, P], F32)
             for b2 in range(2):
                 for hh in range(2):
-                    nc.tensor.transpose(pps[:, b2, hh, :], st32[:, 2 * pair + b2, hh : NODES // 2 : 2], ident[:])
+                    nc.tensor.transpose(pps[:, b2, hh, :], st32[:, b2, hh : NODES // 2 : 2], ident[:])
             prev_tiles[(g, pair)] = pps
 
         def candidate_passes(g, bq, s):
@@ -298,7 +301,7 @@ def tile_gcrnncell_pb_t_kernel(
                 nc.vector.tensor_tensor(
                     out=gated[:],
                     in0=diffs[bq][:],
-                    in1=u_tiles[g][:, bq, :].rearrange("p (x j) -> p x j", j=UNITS),
+                    in1=u_tiles[(g, pair)][:, bq % 2, :].rearrange("p (x j) -> p x j", j=UNITS),
                     op=ALU.mult,
                 )
                 gateds[bq] = gated
@@ -310,27 +313,19 @@ def tile_gcrnncell_pb_t_kernel(
                     in_=z[:].rearrange("p x j -> p (x j)"),
                 )
 
-        load_r(0)
+        load_for_step(-R_LEAD)
+        load_for_step(-R_LEAD + 1)
         load_support_words(0, support0_words)
-        load_support_scales(0, support0_scales, nc.sync, I32)
-        load_r(1)
-        load_h(0)
+        load_support_scales(0, support0_scales, nc.scalar, F32)
+        load_for_step(-R_LEAD + 2)
+        load_for_step(-R_LEAD + 3)
         load_support_words(1, support1_words)
         load_support_scales(1, support1_scales, nc.gpsimd, F32)
         load_c_kernel_scales(nc.gpsimd, F32)
-        load_r(2)
         load_c_kernel_words()
-        load_blend_inputs(0)
-        load_h(1)
         for step in range(-R_LEAD, 2 * N_GROUPS):
             g, i = divmod(step, 2)
-            if i == 0 and g >= -1:
-                if in_range(g + 4):
-                    load_r(g + 4)
-                if in_range(g + 3):
-                    load_h(g + 3)
-                if in_range(g + 2):
-                    load_blend_inputs(g + 2)
+            load_for_step(step + LOAD_AHEAD)
             for bq in (2 * i, 2 * i + 1):
                 for s in range(2):
                     if in_range(g + 1):

@@ -13,19 +13,23 @@ TANH = mybir.ActivationFunctionType.Tanh
 ALU = mybir.AluOpType
 
 P = 128
+HALF = P // 2
 PACK = 4
 BATCH = 32
 NODES = 512
 UNITS = 128
 FEATS = 256
+SUPPORTS = 2
 GROUP = 4
 N_GROUPS = BATCH // GROUP
 QUAD = P // GROUP
 NODE_TILES = NODES // P
+ROW_WORDS = NODES // 2
+LIVE = 4
+H_SCALE_ROWS = FEATS // 32
 R_LEAD = 5
-LOAD_AHEAD = 4
 
-FLOPS = 2 * BATCH * UNITS * NODES * NODES * 2 + 2 * BATCH * NODES * (FEATS + 2 * UNITS) * UNITS
+FLOPS = 2 * BATCH * UNITS * NODES * NODES * SUPPORTS + 2 * BATCH * NODES * (FEATS + SUPPORTS * UNITS) * UNITS
 
 
 def tile_gcrnncell_pb_t_kernel(
@@ -46,7 +50,8 @@ def tile_gcrnncell_pb_t_kernel(
     with ExitStack() as stack:
         stack.enter_context(tc.manual_schedule())
         const = stack.enter_context(tc.tile_pool(name="const", bufs=1))
-        loads = stack.enter_context(tc.tile_pool(name="loads", bufs=LOAD_AHEAD + 3))
+        loads = stack.enter_context(tc.tile_pool(name="loads", bufs=3))
+        gates = stack.enter_context(tc.tile_pool(name="gates", bufs=4))
         work = stack.enter_context(tc.tile_pool(name="work", bufs=2))
         cpool = stack.enter_context(tc.tile_pool(name="cpool", bufs=4))
         hpool = stack.enter_context(tc.tile_pool(name="hpool", bufs=8))
@@ -59,9 +64,13 @@ def tile_gcrnncell_pb_t_kernel(
         ident = const.tile([P, P], F32)
         make_identity(nc, ident[:])
 
+        warm = const.tile([P, 1], F32)
+        nc.vector.memset(warm[:], 0.0)
+        nc.scalar.activation(out=warm[:], in_=warm[:], func=TANH)
+
         w_words = []
         w_plane = []
-        for i in range(2):
+        for i in range(SUPPORTS):
             words = const.tile([P, NODES * PACK], U8, align_bytes=64, name="w_words%d" % i)
             plane = const.tile([P, NODES], U8, align_bytes=64, name="w_plane%d" % i)
             nc.vector.memset(plane[:].bitcast(I32), 0)
@@ -69,8 +78,8 @@ def tile_gcrnncell_pb_t_kernel(
             w_plane.append(plane)
         ckh_words = const.tile([P, 2, UNITS * PACK], U8, align_bytes=64)
         ckh_plane = const.tile([P, 2, UNITS], U8, align_bytes=64)
-        ckd_words = const.tile([P, 2, GROUP, UNITS * PACK], U8, align_bytes=64)
-        ckd_plane = const.tile([P, 2, GROUP, UNITS], U8, align_bytes=64)
+        ckd_words = const.tile([P, SUPPORTS, GROUP, UNITS * PACK], U8, align_bytes=64)
+        ckd_plane = const.tile([P, SUPPORTS, GROUP, UNITS], U8, align_bytes=64)
         nc.vector.memset(ckh_words[:].bitcast(I32), 0)
         nc.vector.memset(ckh_plane[:].bitcast(I32), 0)
         nc.vector.memset(ckd_words[:].bitcast(I32), 0)
@@ -87,34 +96,41 @@ def tile_gcrnncell_pb_t_kernel(
 
         def load_support_scales(i, scales_in, queue, view):
             rows = scales_in[0].bitcast(view)
-            for q in range(4):
-                load_scale_rows(queue, view, w_plane[i][QUAD * q : QUAD * q + 4, :], rows[4 * q : 4 * q + 4, :])
+            for quad in range(P // QUAD):
+                load_scale_rows(
+                    queue,
+                    view,
+                    w_plane[i][QUAD * quad : QUAD * quad + LIVE, :],
+                    rows[LIVE * quad : LIVE * quad + LIVE, :],
+                )
 
         def load_c_kernel_words():
             words_in = c_kernel_words[0].rearrange("p n t -> p (n t)").bitcast(I32)
             for half in range(2):
                 nc.sync.dma_start(
-                    out=ckh_words[64 * half : 64 * half + 64, half, :].bitcast(I32),
-                    in_=words_in[0:64, :],
+                    out=ckh_words[HALF * half : HALF * half + HALF, half, :].bitcast(I32),
+                    in_=words_in[0:HALF, :],
                 )
             for bq in range(GROUP):
                 nc.sync.dma_start(
                     out=ckd_words[QUAD * bq : QUAD * bq + QUAD, :, bq, :].bitcast(I32),
-                    in_=words_in[64:P, :].rearrange("(i a) w -> a i w", i=2),
+                    in_=words_in[HALF:P, :].rearrange("(i a) c -> a i c", i=SUPPORTS),
                 )
 
         def load_c_kernel_scales(queue, view):
             rows = c_kernel_scales[0].bitcast(view)
             for half in range(2):
-                for q in range(2):
-                    base = 64 * half + QUAD * q
-                    load_scale_rows(queue, view, ckh_plane[base : base + 4, half, :], rows[4 * q : 4 * q + 4, :])
+                for quad in range(HALF // QUAD):
+                    base = HALF * half + QUAD * quad
+                    load_scale_rows(
+                        queue, view, ckh_plane[base : base + LIVE, half, :], rows[LIVE * quad : LIVE * quad + LIVE, :]
+                    )
             for bq in range(GROUP):
                 load_scale_rows(
                     queue,
                     view,
-                    ckd_plane[QUAD * bq : QUAD * bq + 4, :, bq, :],
-                    rows[8:16, :].rearrange("(i r) w -> r i w", i=2),
+                    ckd_plane[QUAD * bq : QUAD * bq + LIVE, :, bq, :],
+                    rows[H_SCALE_ROWS : 2 * H_SCALE_ROWS, :].rearrange("(i r) c -> r i c", i=SUPPORTS),
                 )
 
         r_tiles = {}
@@ -130,51 +146,49 @@ def tile_gcrnncell_pb_t_kernel(
         prev_tiles = {}
         cps_tiles = {}
         cand_tiles = {}
+        diff_tiles = {}
 
         def in_range(g):
             return 0 <= g < N_GROUPS
 
-        def load_for_step(step):
-            g, tp = divmod(step + R_LEAD, 2)
-            if in_range(g):
-                r_sb = loads.tile([P, 2, NODES], BF16)
-                rows = r_prev[GROUP * g : GROUP * (g + 1)].rearrange("b (a t) n -> (b a) t n", t=PACK)
-                nc.sync.dma_start(out=r_sb[:], in_=rows[:, 2 * tp : 2 * tp + 2, :])
-                r_tiles[(g, tp)] = r_sb
-            g, pair = divmod(step + 2, 2)
-            if in_range(g):
-                b0 = GROUP * g + 2 * pair
-                h_sb = loads.tile([P, 2, NODE_TILES * FEATS], BF16)
-                nc.sync.dma_start(
-                    out=h_sb[:], in_=h_diff[b0 : b0 + 2].rearrange("b (p x) c -> p b (x c)", x=NODE_TILES)
-                )
-                h_tiles[(g, pair)] = h_sb
-            g, pair = divmod(step, 2)
-            if in_range(g):
-                b0 = GROUP * g + 2 * pair
-                st_sb = loads.tile([P, 2, NODES], BF16)
-                nc.sync.dma_start(out=st_sb[:], in_=state[b0 : b0 + 2].rearrange("b (j m) -> j b m", m=NODES))
-                st_tiles[(g, pair)] = st_sb
-            g, pair = divmod(step - 1, 2)
-            if in_range(g):
-                b0 = GROUP * g + 2 * pair
-                u_sb = loads.tile([P, 2, NODE_TILES * UNITS], BF16)
-                nc.sync.dma_start(
-                    out=u_sb[:], in_=u[b0 : b0 + 2].rearrange("b (p x) j -> p b (x j)", x=NODE_TILES)
-                )
-                u_tiles[(g, pair)] = u_sb
+        def load_r(g):
+            r_sb = loads.tile([P, PACK, NODES], BF16)
+            nc.sync.dma_start(
+                out=r_sb[:], in_=r_prev[GROUP * g : GROUP * (g + 1)].rearrange("b (a t) n -> (b a) t n", t=PACK)
+            )
+            r_tiles[g] = r_sb
 
-        def transpose_r(g, tp):
-            if tp == 0:
+        def load_h(g):
+            h_sb = loads.tile([P, GROUP, NODE_TILES * FEATS], BF16)
+            nc.sync.dma_start(
+                out=h_sb[:],
+                in_=h_diff[GROUP * g : GROUP * (g + 1)].rearrange("b (p x) c -> p b (x c)", x=NODE_TILES),
+            )
+            h_tiles[g] = h_sb
+
+        def load_blend_inputs(g):
+            st_sb = gates.tile([P, GROUP, NODES], BF16)
+            nc.sync.dma_start(
+                out=st_sb[:], in_=state[GROUP * g : GROUP * (g + 1)].rearrange("b (j m) -> j b m", m=NODES)
+            )
+            st_tiles[g] = st_sb
+            u_sb = gates.tile([P, GROUP, NODE_TILES * UNITS], BF16)
+            nc.sync.dma_start(
+                out=u_sb[:], in_=u[GROUP * g : GROUP * (g + 1)].rearrange("b (p x) j -> p b (x j)", x=NODE_TILES)
+            )
+            u_tiles[g] = u_sb
+
+        def transpose_r(g, bank):
+            if bank == 0:
                 rg = work.tile([P, PACK, P, PACK], BF16, align_bytes=64)
                 rg_tiles[g] = rg
-            r32 = r_tiles[(g, tp)][:].bitcast(F32)
+            r32 = r_tiles[g][:].bitcast(F32)
             rg32 = rg_tiles[g][:].bitcast(F32)
             tps = psum_t.tile([P, 2, 2, P], F32)
             for t2 in range(2):
                 for w in range(2):
-                    nc.tensor.transpose(tps[:, t2, w, :], r32[:, t2, w : NODES // 2 : 2], ident[:])
-            nc.scalar.copy(out=rg32[:, 2 * tp : 2 * tp + 2, :, :], in_=tps[:].rearrange("p t w c -> p t c w"))
+                    nc.tensor.transpose(tps[:, t2, w, :], r32[:, 2 * bank + t2, w:ROW_WORDS:2], ident[:])
+            nc.scalar.copy(out=rg32[:, 2 * bank : 2 * bank + 2, :, :], in_=tps[:].rearrange("p t w c -> p t c w"))
 
         def quantise_r(g):
             rq_words = work.tile([P, PACK * P], U32, align_bytes=64)
@@ -182,13 +196,13 @@ def tile_gcrnncell_pb_t_kernel(
             nc.vector.quantize_mx(
                 out=rq_words[:].bitcast(FP8X4),
                 scales=rq_plane[:],
-                in_=rg_tiles[g][:].rearrange("p t c j -> p (t c j)"),
+                in_=rg_tiles[g][:].rearrange("p t c v -> p (t c v)"),
             )
             rq_tiles[g] = (rq_words, rq_plane)
 
-        def diffuse_bank(g, i, m):
+        def diffuse_bank(g, i, span):
             rq_words, rq_plane = rq_tiles[g]
-            if m == 0:
+            if span == 0:
                 cg = work.tile([P, NODE_TILES, P, PACK], BF16, align_bytes=64)
                 cg_tiles[(g, i)] = cg
             dps = psum_d.tile([P, PACK, P], F32)
@@ -197,13 +211,13 @@ def tile_gcrnncell_pb_t_kernel(
                     out=dps[:, t, :],
                     lhsT=rq_words[:, P * t : P * t + P].bitcast(FP8X4),
                     lhsT_scale=rq_plane[:, P * t : P * t + P],
-                    rhs=w_words[i][:, PACK * P * m : PACK * P * (m + 1)].bitcast(FP8X4),
-                    rhs_scale=w_plane[i][:, P * m : P * m + P],
+                    rhs=w_words[i][:, PACK * P * span : PACK * P * (span + 1)].bitcast(FP8X4),
+                    rhs_scale=w_plane[i][:, P * span : P * span + P],
                     start=True,
                     stop=True,
                 )
             nc.scalar.copy(
-                out=cg_tiles[(g, i)][:, :, QUAD * m : QUAD * m + QUAD, :],
+                out=cg_tiles[(g, i)][:, :, QUAD * span : QUAD * span + QUAD, :],
                 in_=dps[:].rearrange("p t (c x) -> p x c t", x=NODE_TILES),
             )
 
@@ -218,11 +232,11 @@ def tile_gcrnncell_pb_t_kernel(
             cq_tiles[(g, i)] = (cq_words, cq_plane)
 
         def transpose_h(g, bq):
-            h32 = h_tiles[(g, bq // 2)][:].bitcast(F32)
+            h32 = h_tiles[g][:].bitcast(F32)
             tps = psum_t.tile([P, 2, 2, P], F32)
             for s in range(2):
                 for w in range(2):
-                    nc.tensor.transpose(tps[:, s, w, :], h32[:, bq % 2, FEATS * s + w : FEATS * (s + 1) : 2], ident[:])
+                    nc.tensor.transpose(tps[:, s, w, :], h32[:, bq, FEATS * s + w : FEATS * (s + 1) : 2], ident[:])
             hg = work.tile([P, 2, P, PACK], BF16, align_bytes=64, bufs=4)
             if bq % 2 == 0:
                 nc.scalar.copy(out=hg[:].bitcast(F32), in_=tps[:].rearrange("p s w c -> p s c w"))
@@ -236,16 +250,16 @@ def tile_gcrnncell_pb_t_kernel(
             nc.vector.quantize_mx(
                 out=hq_words[:].bitcast(FP8X4),
                 scales=hq_plane[:],
-                in_=hg_tiles[(g, bq)][:].rearrange("p s c j -> p (s c j)"),
+                in_=hg_tiles[(g, bq)][:].rearrange("p s c v -> p (s c v)"),
             )
             hq_tiles[(g, bq)] = (hq_words, hq_plane)
 
         def transpose_state(g, pair):
-            st32 = st_tiles[(g, pair)][:].bitcast(F32)
+            st32 = st_tiles[g][:].bitcast(F32)
             pps = psum_p.tile([P, 2, 2, P], F32)
             for b2 in range(2):
-                for hh in range(2):
-                    nc.tensor.transpose(pps[:, b2, hh, :], st32[:, b2, hh : NODES // 2 : 2], ident[:])
+                for h in range(2):
+                    nc.tensor.transpose(pps[:, b2, h, :], st32[:, 2 * pair + b2, h:ROW_WORDS:2], ident[:])
             prev_tiles[(g, pair)] = pps
 
         def candidate_passes(g, bq, s):
@@ -265,7 +279,7 @@ def tile_gcrnncell_pb_t_kernel(
                     start=True,
                     stop=False,
                 )
-                for i in range(2):
+                for i in range(SUPPORTS):
                     cq_words, cq_plane = cq_tiles[(g, i)]
                     nc.tensor.matmul_mx(
                         out=cps[:, x, :],
@@ -274,7 +288,7 @@ def tile_gcrnncell_pb_t_kernel(
                         rhs=ckd_words[:, i, bq, :].bitcast(FP8X4),
                         rhs_scale=ckd_plane[:, i, bq, :],
                         start=False,
-                        stop=(i == 1),
+                        stop=(i == SUPPORTS - 1),
                     )
 
         def candidate_tanh(g, bq):
@@ -282,11 +296,9 @@ def tile_gcrnncell_pb_t_kernel(
             nc.scalar.activation(out=cand[:], in_=cps_tiles[(g, bq)][:], func=TANH)
             cand_tiles[(g, bq)] = cand
 
-        def blend_and_store(g, pair):
-            batches = (2 * pair, 2 * pair + 1)
+        def blend_subtract(g, pair):
             prev_words = prev_tiles[(g, pair)][:].bitcast(BF16)
-            diffs = {}
-            for bq in batches:
+            for bq in (2 * pair, 2 * pair + 1):
                 diff = blend.tile([P, NODE_TILES, UNITS], F32)
                 nc.vector.tensor_tensor(
                     out=diff[:].rearrange("p (h e) j -> p h e j", e=2),
@@ -294,14 +306,17 @@ def tile_gcrnncell_pb_t_kernel(
                     in1=cand_tiles[(g, bq)][:].rearrange("p (h e) j -> p h e j", e=2),
                     op=ALU.subtract,
                 )
-                diffs[bq] = diff
+                diff_tiles[(g, bq)] = diff
+
+        def blend_gate_and_store(g, pair):
+            batches = (2 * pair, 2 * pair + 1)
             gateds = {}
             for bq in batches:
                 gated = blend.tile([P, NODE_TILES, UNITS], F32)
                 nc.vector.tensor_tensor(
                     out=gated[:],
-                    in0=diffs[bq][:],
-                    in1=u_tiles[(g, pair)][:, bq % 2, :].rearrange("p (x j) -> p x j", j=UNITS),
+                    in0=diff_tiles[(g, bq)][:],
+                    in1=u_tiles[g][:, bq, :].rearrange("p (x j) -> p x j", j=UNITS),
                     op=ALU.mult,
                 )
                 gateds[bq] = gated
@@ -313,19 +328,27 @@ def tile_gcrnncell_pb_t_kernel(
                     in_=z[:].rearrange("p x j -> p (x j)"),
                 )
 
-        load_for_step(-R_LEAD)
-        load_for_step(-R_LEAD + 1)
+        load_r(0)
         load_support_words(0, support0_words)
-        load_support_scales(0, support0_scales, nc.scalar, F32)
-        load_for_step(-R_LEAD + 2)
-        load_for_step(-R_LEAD + 3)
+        load_support_scales(0, support0_scales, nc.sync, I32)
+        load_r(1)
+        load_h(0)
         load_support_words(1, support1_words)
         load_support_scales(1, support1_scales, nc.gpsimd, F32)
         load_c_kernel_scales(nc.gpsimd, F32)
+        load_r(2)
         load_c_kernel_words()
+        load_blend_inputs(0)
+        load_h(1)
         for step in range(-R_LEAD, 2 * N_GROUPS):
             g, i = divmod(step, 2)
-            load_for_step(step + LOAD_AHEAD)
+            if i == 0 and g >= -1:
+                if in_range(g + 4):
+                    load_r(g + 4)
+                if in_range(g + 3):
+                    load_h(g + 3)
+                if in_range(g + 2):
+                    load_blend_inputs(g + 2)
             for bq in (2 * i, 2 * i + 1):
                 for s in range(2):
                     if in_range(g + 1):
@@ -336,9 +359,11 @@ def tile_gcrnncell_pb_t_kernel(
                     candidate_tanh(g, bq)
             before_g, before_i = divmod(step - 1, 2)
             if in_range(before_g):
-                blend_and_store(before_g, before_i)
+                blend_subtract(before_g, before_i)
             if in_range(g + 1):
                 quantise_c(g + 1, i)
+            if in_range(before_g):
+                blend_gate_and_store(before_g, before_i)
             r_g, r_bank = divmod(step + R_LEAD, 2)
             if in_range(r_g):
                 transpose_r(r_g, r_bank)
@@ -351,4 +376,5 @@ def tile_gcrnncell_pb_t_kernel(
                 quantise_h(g + 1, 2 * i + 1)
             if in_range(g):
                 transpose_state(g, i)
-        blend_and_store(N_GROUPS - 1, 1)
+        blend_subtract(N_GROUPS - 1, 1)
+        blend_gate_and_store(N_GROUPS - 1, 1)

@@ -158,13 +158,15 @@ def tile_gcrnncell_pb_t_kernel(
             )
             r_tiles[g] = r_sb
 
-        def load_h(g):
-            h_sb = loads.tile([P, GROUP, NODE_TILES * FEATS], BF16)
+        def load_h(g, first, count):
+            if first == 0:
+                h_sb = loads.tile([P, GROUP, NODE_TILES * FEATS], BF16)
+                h_tiles[g] = h_sb
+            b0 = GROUP * g + first
             nc.sync.dma_start(
-                out=h_sb[:],
-                in_=h_diff[GROUP * g : GROUP * (g + 1)].rearrange("b (p x) c -> p b (x c)", x=NODE_TILES),
+                out=h_tiles[g][:, first : first + count, :],
+                in_=h_diff[b0 : b0 + count].rearrange("b (p x) c -> p b (x c)", x=NODE_TILES),
             )
-            h_tiles[g] = h_sb
 
         def load_blend_inputs(g):
             st_sb = gates.tile([P, GROUP, NODES], BF16)
@@ -178,7 +180,13 @@ def tile_gcrnncell_pb_t_kernel(
             )
             u_tiles[g] = u_sb
 
-        def transpose_r(g, bank):
+        def copy_out(on_scalar, dst, src):
+            if on_scalar:
+                nc.scalar.copy(out=dst, in_=src)
+            else:
+                nc.vector.tensor_copy(out=dst, in_=src)
+
+        def transpose_r(g, bank, on_scalar=True):
             if bank == 0:
                 rg = work.tile([P, PACK, P, PACK], BF16, align_bytes=64)
                 rg_tiles[g] = rg
@@ -188,7 +196,7 @@ def tile_gcrnncell_pb_t_kernel(
             for t2 in range(2):
                 for w in range(2):
                     nc.tensor.transpose(tps[:, t2, w, :], r32[:, 2 * bank + t2, w:ROW_WORDS:2], ident[:])
-            nc.scalar.copy(out=rg32[:, 2 * bank : 2 * bank + 2, :, :], in_=tps[:].rearrange("p t w c -> p t c w"))
+            copy_out(on_scalar, rg32[:, 2 * bank : 2 * bank + 2, :, :], tps[:].rearrange("p t w c -> p t c w"))
 
         def quantise_r(g):
             rq_words = work.tile([P, PACK * P], U32, align_bytes=64)
@@ -200,7 +208,7 @@ def tile_gcrnncell_pb_t_kernel(
             )
             rq_tiles[g] = (rq_words, rq_plane)
 
-        def diffuse_bank(g, i, span):
+        def diffuse_bank(g, i, span, on_scalar=True):
             rq_words, rq_plane = rq_tiles[g]
             if span == 0:
                 cg = work.tile([P, NODE_TILES, P, PACK], BF16, align_bytes=64)
@@ -216,9 +224,10 @@ def tile_gcrnncell_pb_t_kernel(
                     start=True,
                     stop=True,
                 )
-            nc.scalar.copy(
-                out=cg_tiles[(g, i)][:, :, QUAD * span : QUAD * span + QUAD, :],
-                in_=dps[:].rearrange("p t (c x) -> p x c t", x=NODE_TILES),
+            copy_out(
+                on_scalar,
+                cg_tiles[(g, i)][:, :, QUAD * span : QUAD * span + QUAD, :],
+                dps[:].rearrange("p t (c x) -> p x c t", x=NODE_TILES),
             )
 
         def quantise_c(g, i):
@@ -238,10 +247,7 @@ def tile_gcrnncell_pb_t_kernel(
                 for w in range(2):
                     nc.tensor.transpose(tps[:, s, w, :], h32[:, bq, FEATS * s + w : FEATS * (s + 1) : 2], ident[:])
             hg = work.tile([P, 2, P, PACK], BF16, align_bytes=64, bufs=4)
-            if bq % 2 == 0:
-                nc.scalar.copy(out=hg[:].bitcast(F32), in_=tps[:].rearrange("p s w c -> p s c w"))
-            else:
-                nc.vector.tensor_copy(out=hg[:].bitcast(F32), in_=tps[:].rearrange("p s w c -> p s c w"))
+            copy_out(bq % 2 == 0, hg[:].bitcast(F32), tps[:].rearrange("p s w c -> p s c w"))
             hg_tiles[(g, bq)] = hg
 
         def quantise_h(g, bq):
@@ -296,9 +302,9 @@ def tile_gcrnncell_pb_t_kernel(
             nc.scalar.activation(out=cand[:], in_=cps_tiles[(g, bq)][:], func=TANH)
             cand_tiles[(g, bq)] = cand
 
-        def blend_subtract(g, pair):
-            prev_words = prev_tiles[(g, pair)][:].bitcast(BF16)
-            for bq in (2 * pair, 2 * pair + 1):
+        def blend_subtract(g, batches):
+            for bq in batches:
+                prev_words = prev_tiles[(g, bq // 2)][:].bitcast(BF16)
                 diff = blend.tile([P, NODE_TILES, UNITS], F32)
                 nc.vector.tensor_tensor(
                     out=diff[:].rearrange("p (h e) j -> p h e j", e=2),
@@ -308,8 +314,7 @@ def tile_gcrnncell_pb_t_kernel(
                 )
                 diff_tiles[(g, bq)] = diff
 
-        def blend_gate_and_store(g, pair):
-            batches = (2 * pair, 2 * pair + 1)
+        def blend_gate_and_store(g, batches, on_vector=()):
             gateds = {}
             for bq in batches:
                 gated = blend.tile([P, NODE_TILES, UNITS], F32)
@@ -322,7 +327,8 @@ def tile_gcrnncell_pb_t_kernel(
                 gateds[bq] = gated
             for bq in batches:
                 z = blend.tile([P, NODE_TILES, UNITS], F32)
-                nc.gpsimd.tensor_tensor(out=z[:], in0=gateds[bq][:], in1=cand_tiles[(g, bq)][:], op=ALU.add)
+                adder = nc.vector if bq in on_vector else nc.gpsimd
+                adder.tensor_tensor(out=z[:], in0=gateds[bq][:], in1=cand_tiles[(g, bq)][:], op=ALU.add)
                 nc.sync.dma_start(
                     out=out[GROUP * g + bq].rearrange("(p f) -> p f", f=NODE_TILES * UNITS),
                     in_=z[:].rearrange("p x j -> p (x j)"),
@@ -331,39 +337,74 @@ def tile_gcrnncell_pb_t_kernel(
         load_r(0)
         load_support_words(0, support0_words)
         load_support_scales(0, support0_scales, nc.sync, I32)
-        load_r(1)
-        load_h(0)
         load_support_words(1, support1_words)
         load_support_scales(1, support1_scales, nc.gpsimd, F32)
         load_c_kernel_scales(nc.gpsimd, F32)
-        load_r(2)
+        load_h(0, 0, 2)
         load_c_kernel_words()
+        load_r(1)
+        load_h(0, 2, 2)
+        load_r(2)
+        load_h(1, 0, GROUP)
         load_blend_inputs(0)
-        load_h(1)
-        for step in range(-R_LEAD, 2 * N_GROUPS):
+        load_r(3)
+        load_h(2, 0, GROUP)
+        load_blend_inputs(1)
+
+        transpose_r(0, 0, on_scalar=False)
+        transpose_r(0, 1)
+        quantise_r(0)
+        for d_i in range(SUPPORTS):
+            for span in range(NODE_TILES):
+                diffuse_bank(0, d_i, span, on_scalar=span % 2 == 1)
+            quantise_c(0, d_i)
+        transpose_h(0, 0)
+        transpose_h(0, 1)
+        quantise_h(0, 0)
+        quantise_h(0, 1)
+        transpose_r(1, 0, on_scalar=False)
+        transpose_r(1, 1)
+        quantise_r(1)
+        transpose_h(0, 2)
+        transpose_h(0, 3)
+        quantise_h(0, 2)
+        quantise_h(0, 3)
+        transpose_r(2, 0)
+
+        for step in range(2 * N_GROUPS):
             g, i = divmod(step, 2)
-            if i == 0 and g >= -1:
+            if i == 0:
                 if in_range(g + 4):
                     load_r(g + 4)
                 if in_range(g + 3):
-                    load_h(g + 3)
+                    load_h(g + 3, 0, GROUP)
                 if in_range(g + 2):
                     load_blend_inputs(g + 2)
-            for bq in (2 * i, 2 * i + 1):
+            pair = (2 * i, 2 * i + 1)
+            last = step == 2 * N_GROUPS - 1
+            before_g, before_i = divmod(step - 1, 2)
+            before_pair = (2 * before_i, 2 * before_i + 1)
+            if last:
+                blend_subtract(before_g, before_pair)
+                transpose_state(g, i)
+                blend_gate_and_store(before_g, before_pair)
+            for bq in pair:
                 for s in range(2):
                     if in_range(g + 1):
                         diffuse_bank(g + 1, i, 2 * (bq % 2) + s)
-                    if in_range(g):
-                        candidate_passes(g, bq, s)
-                if in_range(g):
-                    candidate_tanh(g, bq)
-            before_g, before_i = divmod(step - 1, 2)
+                    candidate_passes(g, bq, s)
+                candidate_tanh(g, bq)
+                if last:
+                    blend_subtract(g, (bq,))
+                    blend_gate_and_store(g, (bq,), on_vector=pair)
+            if last:
+                continue
             if in_range(before_g):
-                blend_subtract(before_g, before_i)
+                blend_subtract(before_g, before_pair)
             if in_range(g + 1):
                 quantise_c(g + 1, i)
             if in_range(before_g):
-                blend_gate_and_store(before_g, before_i)
+                blend_gate_and_store(before_g, before_pair)
             r_g, r_bank = divmod(step + R_LEAD, 2)
             if in_range(r_g):
                 transpose_r(r_g, r_bank)
@@ -374,7 +415,4 @@ def tile_gcrnncell_pb_t_kernel(
                 transpose_h(g + 1, 2 * i + 1)
                 quantise_h(g + 1, 2 * i)
                 quantise_h(g + 1, 2 * i + 1)
-            if in_range(g):
-                transpose_state(g, i)
-        blend_subtract(N_GROUPS - 1, 1)
-        blend_gate_and_store(N_GROUPS - 1, 1)
+            transpose_state(g, i)

@@ -68,6 +68,8 @@ def tile_gcrnncell_pb_t_kernel(
         nc.vector.memset(warm[:], 0.0)
         nc.scalar.activation(out=warm[:], in_=warm[:], func=TANH)
 
+        ck_plane = const.tile([P, 1 + SUPPORTS, UNITS], U8, align_bytes=64)
+        nc.vector.memset(ck_plane[:].bitcast(I32), 0)
         w_words = []
         w_plane = []
         for i in range(SUPPORTS):
@@ -77,13 +79,9 @@ def tile_gcrnncell_pb_t_kernel(
             w_words.append(words)
             w_plane.append(plane)
         ckh_words = const.tile([P, 2, UNITS * PACK], U8, align_bytes=64)
-        ckh_plane = const.tile([P, 2, UNITS], U8, align_bytes=64)
         ckd_words = const.tile([P, SUPPORTS, GROUP, UNITS * PACK], U8, align_bytes=64)
-        ckd_plane = const.tile([P, SUPPORTS, GROUP, UNITS], U8, align_bytes=64)
         nc.vector.memset(ckh_words[:].bitcast(I32), 0)
-        nc.vector.memset(ckh_plane[:].bitcast(I32), 0)
         nc.vector.memset(ckd_words[:].bitcast(I32), 0)
-        nc.vector.memset(ckd_plane[:].bitcast(I32), 0)
 
         def load_support_words(i, words_in):
             nc.sync.dma_start(
@@ -91,15 +89,13 @@ def tile_gcrnncell_pb_t_kernel(
                 in_=words_in[0].rearrange("p n t -> p (n t)").bitcast(I32),
             )
 
-        def load_scale_rows(queue, view, plane_rows, rows):
-            queue.dma_start(out=plane_rows.bitcast(view), in_=rows)
+        def load_scale_rows(plane_rows, rows):
+            nc.sync.dma_start(out=plane_rows.bitcast(I32), in_=rows)
 
-        def load_support_scales(i, scales_in, queue, view):
-            rows = scales_in[0].bitcast(view)
+        def load_support_scales(i, scales_in):
+            rows = scales_in[0].bitcast(I32)
             for quad in range(P // QUAD):
                 load_scale_rows(
-                    queue,
-                    view,
                     w_plane[i][QUAD * quad : QUAD * quad + LIVE, :],
                     rows[LIVE * quad : LIVE * quad + LIVE, :],
                 )
@@ -117,21 +113,17 @@ def tile_gcrnncell_pb_t_kernel(
                     in_=words_in[HALF:P, :].rearrange("(i a) c -> a i c", i=SUPPORTS),
                 )
 
-        def load_c_kernel_scales(queue, view):
-            rows = c_kernel_scales[0].bitcast(view)
-            for half in range(2):
-                for quad in range(HALF // QUAD):
-                    base = HALF * half + QUAD * quad
+        def load_c_kernel_scales():
+            rows = c_kernel_scales[0].bitcast(I32)
+            for quad in range(P // QUAD):
+                live = ck_plane[QUAD * quad : QUAD * quad + LIVE, :, :]
+                if quad % 2 == 0:
+                    load_scale_rows(live[:, 0, :], rows[0:LIVE, :])
                     load_scale_rows(
-                        queue, view, ckh_plane[base : base + LIVE, half, :], rows[LIVE * quad : LIVE * quad + LIVE, :]
+                        live[:, 1:, :], rows[H_SCALE_ROWS:, :].rearrange("(k r) c -> r k c", r=LIVE)
                     )
-            for bq in range(GROUP):
-                load_scale_rows(
-                    queue,
-                    view,
-                    ckd_plane[QUAD * bq : QUAD * bq + LIVE, :, bq, :],
-                    rows[H_SCALE_ROWS : 2 * H_SCALE_ROWS, :].rearrange("(i r) c -> r i c", i=SUPPORTS),
-                )
+                else:
+                    load_scale_rows(live, rows[LIVE:, :].rearrange("(k r) c -> r k c", r=LIVE))
 
         r_tiles = {}
         h_tiles = {}
@@ -208,12 +200,12 @@ def tile_gcrnncell_pb_t_kernel(
             )
             rq_tiles[g] = (rq_words, rq_plane)
 
-        def diffuse_bank(g, i, span, on_scalar=True):
+        def diffuse_bank(g, i, span, on_scalar=True, pool=psum_d, tag="dps"):
             rq_words, rq_plane = rq_tiles[g]
             if span == 0:
                 cg = work.tile([P, NODE_TILES, P, PACK], BF16, align_bytes=64)
                 cg_tiles[(g, i)] = cg
-            dps = psum_d.tile([P, PACK, P], F32)
+            dps = pool.tile([P, PACK, P], F32, name=tag)
             for t in range(PACK):
                 nc.tensor.matmul_mx(
                     out=dps[:, t, :],
@@ -260,9 +252,9 @@ def tile_gcrnncell_pb_t_kernel(
             )
             hq_tiles[(g, bq)] = (hq_words, hq_plane)
 
-        def transpose_state(g, pair):
+        def transpose_state(g, pair, pool=psum_p, tag="pps"):
             st32 = st_tiles[g][:].bitcast(F32)
-            pps = psum_p.tile([P, 2, 2, P], F32)
+            pps = pool.tile([P, 2, 2, P], F32, name=tag)
             for b2 in range(2):
                 for h in range(2):
                     nc.tensor.transpose(pps[:, b2, h, :], st32[:, 2 * pair + b2, h:ROW_WORDS:2], ident[:])
@@ -281,7 +273,7 @@ def tile_gcrnncell_pb_t_kernel(
                     lhsT=hq_words[:, P * s : P * s + P].bitcast(FP8X4),
                     lhsT_scale=hq_plane[:, P * s : P * s + P],
                     rhs=ckh_words[:, half, :].bitcast(FP8X4),
-                    rhs_scale=ckh_plane[:, half, :],
+                    rhs_scale=ck_plane[:, 0, :],
                     start=True,
                     stop=False,
                 )
@@ -292,7 +284,7 @@ def tile_gcrnncell_pb_t_kernel(
                         lhsT=cq_words[:, P * x : P * x + P].bitcast(FP8X4),
                         lhsT_scale=cq_plane[:, P * x : P * x + P],
                         rhs=ckd_words[:, i, bq, :].bitcast(FP8X4),
-                        rhs_scale=ckd_plane[:, i, bq, :],
+                        rhs_scale=ck_plane[:, 1 + i, :],
                         start=False,
                         stop=(i == SUPPORTS - 1),
                     )
@@ -335,14 +327,14 @@ def tile_gcrnncell_pb_t_kernel(
                 )
 
         load_r(0)
+        load_support_scales(0, support0_scales)
         load_support_words(0, support0_words)
-        load_support_scales(0, support0_scales, nc.sync, I32)
-        load_support_words(1, support1_words)
-        load_support_scales(1, support1_scales, nc.gpsimd, F32)
-        load_c_kernel_scales(nc.gpsimd, F32)
         load_h(0, 0, 2)
-        load_c_kernel_words()
+        load_support_words(1, support1_words)
+        load_support_scales(1, support1_scales)
         load_r(1)
+        load_c_kernel_scales()
+        load_c_kernel_words()
         load_h(0, 2, 2)
         load_r(2)
         load_h(1, 0, GROUP)
@@ -355,15 +347,17 @@ def tile_gcrnncell_pb_t_kernel(
         transpose_r(0, 1)
         quantise_r(0)
         for d_i in range(SUPPORTS):
-            for span in range(NODE_TILES):
-                diffuse_bank(0, d_i, span, on_scalar=span % 2 == 1)
+            for span in range(0, NODE_TILES, 2):
+                diffuse_bank(0, d_i, span, on_scalar=False)
+                diffuse_bank(0, d_i, span + 1, pool=psum_c, tag="cps")
+                if d_i == 0:
+                    transpose_h(0, span // 2)
+                else:
+                    transpose_r(1, span // 2, on_scalar=span == 0)
             quantise_c(0, d_i)
-        transpose_h(0, 0)
-        transpose_h(0, 1)
-        quantise_h(0, 0)
-        quantise_h(0, 1)
-        transpose_r(1, 0, on_scalar=False)
-        transpose_r(1, 1)
+            if d_i == 0:
+                quantise_h(0, 0)
+                quantise_h(0, 1)
         quantise_r(1)
         transpose_h(0, 2)
         transpose_h(0, 3)
@@ -386,7 +380,6 @@ def tile_gcrnncell_pb_t_kernel(
             before_pair = (2 * before_i, 2 * before_i + 1)
             if last:
                 blend_subtract(before_g, before_pair)
-                transpose_state(g, i)
                 blend_gate_and_store(before_g, before_pair)
             for bq in pair:
                 for s in range(2):
@@ -416,3 +409,5 @@ def tile_gcrnncell_pb_t_kernel(
                 quantise_h(g + 1, 2 * i)
                 quantise_h(g + 1, 2 * i + 1)
             transpose_state(g, i)
+            if step == 2 * N_GROUPS - 2:
+                transpose_state(g, 1, psum_t, "tps")

from contextlib import ExitStack

import concourse.mybir as mybir
from concourse.masks import make_identity

F32 = mybir.dt.float32
BF16 = mybir.dt.bfloat16
I32 = mybir.dt.int32
U32 = mybir.dt.uint32
U8 = mybir.dt.uint8
FP8X4 = mybir.dt.float8_e4m3fn_x4
TANH = mybir.ActivationFunctionType.Tanh
ALU = mybir.AluOpType

P = 128
HALF = P // 2
PACK = 4
BATCH = 32
NODES = 512
UNITS = 128
FEATS = 256
SUPPORTS = 2
GROUP = 4
N_GROUPS = BATCH // GROUP
QUAD = P // GROUP
NODE_TILES = NODES // P
ROW_WORDS = NODES // 2
LIVE = 4
H_SCALE_ROWS = FEATS // 32
R_LEAD = 5

FLOPS = 2 * BATCH * UNITS * NODES * NODES * SUPPORTS + 2 * BATCH * NODES * (FEATS + SUPPORTS * UNITS) * UNITS


def tile_gcrnncell_pb_t_kernel(
    tc,
    r_prev,
    h_diff,
    u,
    state,
    support0_words,
    support0_scales,
    support1_words,
    support1_scales,
    c_kernel_words,
    c_kernel_scales,
    out,
):
    nc = tc.nc
    with ExitStack() as stack:
        stack.enter_context(tc.manual_schedule())
        const = stack.enter_context(tc.tile_pool(name="const", bufs=1))
        loads = stack.enter_context(tc.tile_pool(name="loads", bufs=3))
        gates = stack.enter_context(tc.tile_pool(name="gates", bufs=4))
        work = stack.enter_context(tc.tile_pool(name="work", bufs=2))
        cpool = stack.enter_context(tc.tile_pool(name="cpool", bufs=4))
        hpool = stack.enter_context(tc.tile_pool(name="hpool", bufs=8))
        blend = stack.enter_context(tc.tile_pool(name="blend", bufs=5))
        psum_t = stack.enter_context(tc.psum_pool(name="psum_t", bufs=3))
        psum_d = stack.enter_context(tc.psum_pool(name="psum_d", bufs=2))
        psum_c = stack.enter_context(tc.psum_pool(name="psum_c", bufs=2))
        psum_p = stack.enter_context(tc.psum_pool(name="psum_p", bufs=1))

        ident = const.tile([P, P], F32)
        make_identity(nc, ident[:])

        warm = const.tile([P, 1], F32)
        nc.vector.memset(warm[:], 0.0)
        nc.scalar.activation(out=warm[:], in_=warm[:], func=TANH)

        ck_plane = const.tile([P, 1 + SUPPORTS, UNITS], U8, align_bytes=64)
        nc.vector.memset(ck_plane[:].bitcast(I32), 0)
        w_words = []
        w_plane = []
        for i in range(SUPPORTS):
            words = const.tile([P, NODES * PACK], U8, align_bytes=64, name="w_words%d" % i)
            plane = const.tile([P, NODES], U8, align_bytes=64, name="w_plane%d" % i)
            nc.vector.memset(plane[:].bitcast(I32), 0)
            w_words.append(words)
            w_plane.append(plane)
        ckh_words = const.tile([P, 2, UNITS * PACK], U8, align_bytes=64)
        ckd_words = const.tile([P, SUPPORTS, GROUP, UNITS * PACK], U8, align_bytes=64)
        nc.vector.memset(ckh_words[:].bitcast(I32), 0)
        nc.vector.memset(ckd_words[:].bitcast(I32), 0)

        def load_support_words(i, words_in):
            nc.sync.dma_start(
                out=w_words[i][:].bitcast(I32),
                in_=words_in[0].rearrange("p n t -> p (n t)").bitcast(I32),
            )

        def load_scale_rows(plane_rows, rows):
            nc.sync.dma_start(out=plane_rows.bitcast(I32), in_=rows)

        def load_support_scales(i, scales_in):
            rows = scales_in[0].bitcast(I32)
            for quad in range(P // QUAD):
                load_scale_rows(
                    w_plane[i][QUAD * quad : QUAD * quad + LIVE, :],
                    rows[LIVE * quad : LIVE * quad + LIVE, :],
                )

        def load_c_kernel_words():
            words_in = c_kernel_words[0].rearrange("p n t -> p (n t)").bitcast(I32)
            for half in range(2):
                nc.sync.dma_start(
                    out=ckh_words[HALF * half : HALF * half + HALF, half, :].bitcast(I32),
                    in_=words_in[0:HALF, :],
                )
            for bq in range(GROUP):
                nc.sync.dma_start(
                    out=ckd_words[QUAD * bq : QUAD * bq + QUAD, :, bq, :].bitcast(I32),
                    in_=words_in[HALF:P, :].rearrange("(i a) c -> a i c", i=SUPPORTS),
                )

        def load_c_kernel_scales():
            rows = c_kernel_scales[0].bitcast(I32)
            for quad in range(P // QUAD):
                live = ck_plane[QUAD * quad : QUAD * quad + LIVE, :, :]
                if quad % 2 == 0:
                    load_scale_rows(live[:, 0, :], rows[0:LIVE, :])
                    load_scale_rows(
                        live[:, 1:, :], rows[H_SCALE_ROWS:, :].rearrange("(k r) c -> r k c", r=LIVE)
                    )
                else:
                    load_scale_rows(live, rows[LIVE:, :].rearrange("(k r) c -> r k c", r=LIVE))

        r_tiles = {}
        h_tiles = {}
        u_tiles = {}
        st_tiles = {}
        rg_tiles = {}
        rq_tiles = {}
        cg_tiles = {}
        cq_tiles = {}
        hg_tiles = {}
        hq_tiles = {}
        prev_tiles = {}
        cps_tiles = {}
        cand_tiles = {}
        diff_tiles = {}

        def in_range(g):
            return 0 <= g < N_GROUPS

        def load_r(g):
            r_sb = loads.tile([P, PACK, NODES], BF16)
            nc.sync.dma_start(
                out=r_sb[:], in_=r_prev[GROUP * g : GROUP * (g + 1)].rearrange("b (a t) n -> (b a) t n", t=PACK)
            )
            r_tiles[g] = r_sb

        def load_h(g, first, count):
            if first == 0:
                h_sb = loads.tile([P, GROUP, NODE_TILES * FEATS], BF16)
                h_tiles[g] = h_sb
            b0 = GROUP * g + first
            nc.sync.dma_start(
                out=h_tiles[g][:, first : first + count, :],
                in_=h_diff[b0 : b0 + count].rearrange("b (p x) c -> p b (x c)", x=NODE_TILES),
            )

        def load_blend_inputs(g):
            st_sb = gates.tile([P, GROUP, NODES], BF16)
            nc.sync.dma_start(
                out=st_sb[:], in_=state[GROUP * g : GROUP * (g + 1)].rearrange("b (j m) -> j b m", m=NODES)
            )
            st_tiles[g] = st_sb
            u_sb = gates.tile([P, GROUP, NODE_TILES * UNITS], BF16)
            nc.sync.dma_start(
                out=u_sb[:], in_=u[GROUP * g : GROUP * (g + 1)].rearrange("b (p x) j -> p b (x j)", x=NODE_TILES)
            )
            u_tiles[g] = u_sb

        def copy_out(on_scalar, dst, src):
            if on_scalar:
                nc.scalar.copy(out=dst, in_=src)
            else:
                nc.vector.tensor_copy(out=dst, in_=src)

        def transpose_r(g, bank, on_scalar=True):
            if bank == 0:
                rg = work.tile([P, PACK, P, PACK], BF16, align_bytes=64)
                rg_tiles[g] = rg
            r32 = r_tiles[g][:].bitcast(F32)
            rg32 = rg_tiles[g][:].bitcast(F32)
            tps = psum_t.tile([P, 2, 2, P], F32)
            for t2 in range(2):
                for w in range(2):
                    nc.tensor.transpose(tps[:, t2, w, :], r32[:, 2 * bank + t2, w:ROW_WORDS:2], ident[:])
            copy_out(on_scalar, rg32[:, 2 * bank : 2 * bank + 2, :, :], tps[:].rearrange("p t w c -> p t c w"))

        def quantise_r(g):
            rq_words = work.tile([P, PACK * P], U32, align_bytes=64)
            rq_plane = work.tile([P, PACK * P], U8, align_bytes=64)
            nc.vector.quantize_mx(
                out=rq_words[:].bitcast(FP8X4),
                scales=rq_plane[:],
                in_=rg_tiles[g][:].rearrange("p t c v -> p (t c v)"),
            )
            rq_tiles[g] = (rq_words, rq_plane)

        def diffuse_bank(g, i, span, on_scalar=True, pool=psum_d, tag="dps"):
            rq_words, rq_plane = rq_tiles[g]
            if span == 0:
                cg = work.tile([P, NODE_TILES, P, PACK], BF16, align_bytes=64)
                cg_tiles[(g, i)] = cg
            dps = pool.tile([P, PACK, P], F32, name=tag)
            for t in range(PACK):
                nc.tensor.matmul_mx(
                    out=dps[:, t, :],
                    lhsT=rq_words[:, P * t : P * t + P].bitcast(FP8X4),
                    lhsT_scale=rq_plane[:, P * t : P * t + P],
                    rhs=w_words[i][:, PACK * P * span : PACK * P * (span + 1)].bitcast(FP8X4),
                    rhs_scale=w_plane[i][:, P * span : P * span + P],
                    start=True,
                    stop=True,
                )
            copy_out(
                on_scalar,
                cg_tiles[(g, i)][:, :, QUAD * span : QUAD * span + QUAD, :],
                dps[:].rearrange("p t (c x) -> p x c t", x=NODE_TILES),
            )

        def quantise_c(g, i):
            cq_words = cpool.tile([P, NODES], U32, align_bytes=64)
            cq_plane = cpool.tile([P, NODES], U8, align_bytes=64)
            nc.vector.quantize_mx(
                out=cq_words[:].bitcast(FP8X4),
                scales=cq_plane[:],
                in_=cg_tiles[(g, i)][:].rearrange("p x c t -> p (x c t)"),
            )
            cq_tiles[(g, i)] = (cq_words, cq_plane)

        def transpose_h(g, bq):
            h32 = h_tiles[g][:].bitcast(F32)
            tps = psum_t.tile([P, 2, 2, P], F32)
            for s in range(2):
                for w in range(2):
                    nc.tensor.transpose(tps[:, s, w, :], h32[:, bq, FEATS * s + w : FEATS * (s + 1) : 2], ident[:])
            hg = work.tile([P, 2, P, PACK], BF16, align_bytes=64, bufs=4)
            copy_out(bq % 2 == 0, hg[:].bitcast(F32), tps[:].rearrange("p s w c -> p s c w"))
            hg_tiles[(g, bq)] = hg

        def quantise_h(g, bq):
            hq_words = hpool.tile([P, 2 * P], U32, align_bytes=64)
            hq_plane = hpool.tile([P, 2 * P], U8, align_bytes=64)
            nc.vector.quantize_mx(
                out=hq_words[:].bitcast(FP8X4),
                scales=hq_plane[:],
                in_=hg_tiles[(g, bq)][:].rearrange("p s c v -> p (s c v)"),
            )
            hq_tiles[(g, bq)] = (hq_words, hq_plane)

        def transpose_state(g, pair, pool=psum_p, tag="pps"):
            st32 = st_tiles[g][:].bitcast(F32)
            pps = pool.tile([P, 2, 2, P], F32, name=tag)
            for b2 in range(2):
                for h in range(2):
                    nc.tensor.transpose(pps[:, b2, h, :], st32[:, 2 * pair + b2, h:ROW_WORDS:2], ident[:])
            prev_tiles[(g, pair)] = pps

        def candidate_passes(g, bq, s):
            if s == 0:
                cps = psum_c.tile([P, NODE_TILES, UNITS], F32)
                cps_tiles[(g, bq)] = cps
            cps = cps_tiles[(g, bq)]
            hq_words, hq_plane = hq_tiles[(g, bq)]
            for half in range(2):
                x = 2 * s + half
                nc.tensor.matmul_mx(
                    out=cps[:, x, :],
                    lhsT=hq_words[:, P * s : P * s + P].bitcast(FP8X4),
                    lhsT_scale=hq_plane[:, P * s : P * s + P],
                    rhs=ckh_words[:, half, :].bitcast(FP8X4),
                    rhs_scale=ck_plane[:, 0, :],
                    start=True,
                    stop=False,
                )
                for i in range(SUPPORTS):
                    cq_words, cq_plane = cq_tiles[(g, i)]
                    nc.tensor.matmul_mx(
                        out=cps[:, x, :],
                        lhsT=cq_words[:, P * x : P * x + P].bitcast(FP8X4),
                        lhsT_scale=cq_plane[:, P * x : P * x + P],
                        rhs=ckd_words[:, i, bq, :].bitcast(FP8X4),
                        rhs_scale=ck_plane[:, 1 + i, :],
                        start=False,
                        stop=(i == SUPPORTS - 1),
                    )

        def candidate_tanh(g, bq):
            cand = blend.tile([P, NODE_TILES, UNITS], F32)
            nc.scalar.activation(out=cand[:], in_=cps_tiles[(g, bq)][:], func=TANH)
            cand_tiles[(g, bq)] = cand

        def blend_subtract(g, batches):
            for bq in batches:
                prev_words = prev_tiles[(g, bq // 2)][:].bitcast(BF16)
                diff = blend.tile([P, NODE_TILES, UNITS], F32)
                nc.vector.tensor_tensor(
                    out=diff[:].rearrange("p (h e) j -> p h e j", e=2),
                    in0=prev_words[:, bq % 2].rearrange("p h (j e) -> p h e j", e=2),
                    in1=cand_tiles[(g, bq)][:].rearrange("p (h e) j -> p h e j", e=2),
                    op=ALU.subtract,
                )
                diff_tiles[(g, bq)] = diff

        def blend_gate_and_store(g, batches, on_vector=()):
            gateds = {}
            for bq in batches:
                gated = blend.tile([P, NODE_TILES, UNITS], F32)
                nc.vector.tensor_tensor(
                    out=gated[:],
                    in0=diff_tiles[(g, bq)][:],
                    in1=u_tiles[g][:, bq, :].rearrange("p (x j) -> p x j", j=UNITS),
                    op=ALU.mult,
                )
                gateds[bq] = gated
            for bq in batches:
                z = blend.tile([P, NODE_TILES, UNITS], F32)
                adder = nc.vector if bq in on_vector else nc.gpsimd
                adder.tensor_tensor(out=z[:], in0=gateds[bq][:], in1=cand_tiles[(g, bq)][:], op=ALU.add)
                nc.sync.dma_start(
                    out=out[GROUP * g + bq].rearrange("(p f) -> p f", f=NODE_TILES * UNITS),
                    in_=z[:].rearrange("p x j -> p (x j)"),
                )

        load_r(0)
        load_support_scales(0, support0_scales)
        load_support_words(0, support0_words)
        load_h(0, 0, 2)
        load_support_words(1, support1_words)
        load_support_scales(1, support1_scales)
        load_r(1)
        load_c_kernel_scales()
        load_c_kernel_words()
        load_h(0, 2, 2)
        load_r(2)
        load_h(1, 0, GROUP)
        load_blend_inputs(0)
        load_r(3)
        load_h(2, 0, GROUP)
        load_blend_inputs(1)

        transpose_r(0, 0, on_scalar=False)
        transpose_r(0, 1)
        quantise_r(0)
        for d_i in range(SUPPORTS):
            for span in range(0, NODE_TILES, 2):
                diffuse_bank(0, d_i, span, on_scalar=False)
                diffuse_bank(0, d_i, span + 1, pool=psum_c, tag="cps")
                if d_i == 0:
                    transpose_h(0, span // 2)
                else:
                    transpose_r(1, span // 2, on_scalar=span == 0)
            quantise_c(0, d_i)
            if d_i == 0:
                quantise_h(0, 0)
                quantise_h(0, 1)
        quantise_r(1)
        transpose_h(0, 2)
        transpose_h(0, 3)
        quantise_h(0, 2)
        quantise_h(0, 3)
        transpose_r(2, 0)

        for step in range(2 * N_GROUPS):
            g, i = divmod(step, 2)
            if i == 0:
                if in_range(g + 4):
                    load_r(g + 4)
                if in_range(g + 3):
                    load_h(g + 3, 0, GROUP)
                if in_range(g + 2):
                    load_blend_inputs(g + 2)
            pair = (2 * i, 2 * i + 1)
            last = step == 2 * N_GROUPS - 1
            before_g, before_i = divmod(step - 1, 2)
            before_pair = (2 * before_i, 2 * before_i + 1)
            if last:
                blend_subtract(before_g, before_pair)
                blend_gate_and_store(before_g, before_pair)
            for bq in pair:
                for s in range(2):
                    if in_range(g + 1):
                        diffuse_bank(g + 1, i, 2 * (bq % 2) + s)
                    candidate_passes(g, bq, s)
                candidate_tanh(g, bq)
                if last:
                    blend_subtract(g, (bq,))
                    blend_gate_and_store(g, (bq,), on_vector=pair)
            if last:
                continue
            if in_range(before_g):
                blend_subtract(before_g, before_pair)
            if in_range(g + 1):
                quantise_c(g + 1, i)
            if in_range(before_g):
                blend_gate_and_store(before_g, before_pair)
            r_g, r_bank = divmod(step + R_LEAD, 2)
            if in_range(r_g):
                transpose_r(r_g, r_bank)
                if r_bank == 1:
                    quantise_r(r_g)
            if in_range(g + 1):
                transpose_h(g + 1, 2 * i)
                transpose_h(g + 1, 2 * i + 1)
                quantise_h(g + 1, 2 * i)
                quantise_h(g + 1, 2 * i + 1)
            transpose_state(g, i)
            if step == 2 * N_GROUPS - 2:
                transpose_state(g, 1, psum_t, "tps")
